import numpy as np
import ml_dtypes


def mxq(x, axis, fmt="e4m3"):
    dtype, down = {"e4m3": (ml_dtypes.float8_e4m3fn, 7), "e5m2": (ml_dtypes.float8_e5m2, 14)}[fmt]
    v = np.moveaxis(np.asarray(x, np.float32).astype(ml_dtypes.bfloat16).astype(np.float64), axis, -1)
    blocks = v.reshape(v.shape[:-1] + (-1, 32))
    amax = np.abs(blocks).max(-1, keepdims=True)
    byte = np.maximum(np.where(amax > 0, np.frexp(amax)[1] - 1 + 127, 0) - down, 1)
    scale = np.exp2(byte - 127.0)
    codes = (blocks / scale).astype(np.float32).astype(dtype).astype(np.float64)
    return np.moveaxis((codes * scale).reshape(v.shape), -1, axis)


WIDE = False


def mx_kscale(k):
    if not WIDE:
        return np.ones(k)
    levels = np.array([10, -10, 5, -5, 0])
    a = np.random.permutation(np.resize(levels, k // 512 * 4)).reshape(k // 512, 4)
    idx = np.arange(k)
    return np.exp2(a[idx // 512, idx % 128 // 32])


BF16 = ml_dtypes.bfloat16


def bf(x):
    return np.asarray(x, np.float32).astype(BF16)


def f64(x):
    return np.asarray(x).astype(np.float64)


E2M1 = np.array([0.0, 0.5, 1.0, 1.5, 2.0, 3.0, 4.0, 6.0, -0.0, -0.5, -1.0, -1.5, -2.0, -3.0, -4.0, -6.0])


def pack_weight(w, fmt):
    k, n = w.shape
    w = f64(bf(w)).reshape(k // 32, 32, n)
    amax = np.abs(w).max(1)
    if fmt == "e4m3":
        byte = np.frexp(amax)[1] - 1 + 127 - 7
    else:
        mant, ex = np.frexp(amax / 6.0)
        byte = np.where(mant > 0.5, ex, ex - 1) + 127
    byte = np.clip(np.where(amax > 0, byte, 1), 1, 254)
    scaled = (w * np.exp2(127.0 - byte)[:, None, :]).reshape(k, n).astype(np.float32)
    by_word = np.ascontiguousarray(scaled.reshape(k // 512, 128, 4, n).transpose(0, 1, 3, 2))
    if fmt == "e4m3":
        words = by_word.astype(ml_dtypes.float8_e4m3fn).view(np.uint8)
    else:
        c = by_word.astype(ml_dtypes.float4_e2m1fn).view(np.uint8) & 0xF
        words = c[..., 0::2] | (c[..., 1::2] << 4)
    return np.ascontiguousarray(words), np.ascontiguousarray(byte.astype(np.uint8).reshape(k // 512, 16, n))


def unpack_weight(words, scales, fmt):
    g, p, n, _ = words.shape
    if fmt == "e4m3":
        vals = np.ascontiguousarray(words).view(ml_dtypes.float8_e4m3fn).astype(np.float64)
    else:
        nib = np.empty((g, p, n, 4), np.uint8)
        nib[..., 0::2] = words & 0xF
        nib[..., 1::2] = words >> 4
        vals = E2M1[nib]
    vals = vals * np.repeat(np.exp2(scales.astype(np.float64) - 127.0), 8, axis=1)[..., None]
    return vals.transpose(0, 1, 3, 2).reshape(g * 512, n)


B, D_IN, D_HID, D_OUT = 256, 512, 8192, 512
EPS = 1e-12
NORM_MAX = 16
FMT = "e4m3"


def setup_inputs():
    s, t = mx_kscale(D_IN), mx_kscale(D_HID)
    x = bf(np.random.standard_normal((B, D_IN)))
    in_mean = bf(np.random.standard_normal(D_IN) * 0.1)
    in_std = bf(np.random.uniform(0.5, 1.5, D_IN) / s)
    out_mean = bf(np.random.standard_normal(D_OUT) * 0.1)
    out_std = bf(np.random.uniform(0.5, 1.5, D_OUT))
    W1 = np.random.standard_normal((D_HID, D_IN)) / np.sqrt(D_IN) / s[None, :] * t[:, None]
    b1 = bf(np.random.standard_normal(D_HID) * 0.1 * t)
    W2 = np.random.standard_normal((D_OUT, D_HID)) * 0.85 / np.sqrt(D_HID) / t[None, :]
    b2 = bf(np.random.standard_normal(D_OUT) * 0.1)
    W1_words, W1_scales = pack_weight(np.ascontiguousarray(W1.T), FMT)
    W2_words, W2_scales = pack_weight(np.ascontiguousarray(W2.T), FMT)
    return {
        "x": x,
        "in_mean": in_mean,
        "in_std": in_std,
        "out_mean": out_mean,
        "out_std": out_std,
        "W1_words": W1_words,
        "W1_scales": W1_scales,
        "b1": b1,
        "W2_words": W2_words,
        "W2_scales": W2_scales,
        "b2": b2,
        "norm_max": NORM_MAX,
    }


def reference(x, in_mean, in_std, out_mean, out_std, W1_words, W1_scales, b1, W2_words, W2_scales, b2, norm_max):
    x, in_mean, in_std, out_mean, out_std = f64(x), f64(in_mean), f64(in_std), f64(out_mean), f64(out_std)
    norm_max = float(norm_max)
    x_copy = x[..., :D_OUT]
    xn = (x - in_mean) / in_std
    h = np.maximum((mxq(xn, 1, "e4m3") @ unpack_weight(W1_words, W1_scales, FMT)) + f64(b1), 0.0)
    res = (mxq(h, 1, "e4m3") @ unpack_weight(W2_words, W2_scales, FMT)) + f64(b2)
    norms = np.sqrt((res * res).sum(-1, keepdims=True))
    scale = norm_max / norms
    res = np.where(norms > norm_max, res * scale, res)
    res = res * out_std + out_mean - in_mean
    mapped = res + x_copy
    mnorm = np.sqrt((mapped * mapped).sum(-1, keepdims=True))
    return mapped / np.maximum(mnorm, EPS)

@@ -1,0 +1,283 @@
+from contextlib import ExitStack
+
+import concourse.bass as bass
+import concourse.mybir as mybir
+import concourse.tile as tile
+from concourse.masks import make_identity
+
+F32 = mybir.dt.float32
+BF16 = mybir.dt.bfloat16
+I32 = mybir.dt.int32
+U32 = mybir.dt.uint32
+U8 = mybir.dt.uint8
+FP8X4 = mybir.dt.float8_e4m3fn_x4
+ALU = mybir.AluOpType
+ACT = mybir.ActivationFunctionType
+
+P = 128
+B, D_IN, D_HID, D_OUT = 256, 512, 8192, 512
+NT = B // P
+NG = D_HID // 512
+EPS = 1e-12
+FLOPS = 2 * B * D_IN * D_HID + 2 * B * D_HID * D_OUT
+
+
+def tile_mlp_w_kernel(tc, x, in_mean, in_std, out_mean, out_std, W1_words, W1_scales, b1,
+                                 W2_words, W2_scales, b2, norm_max, out):
+    nc = tc.nc
+    with ExitStack() as ctx:
+        keep = ctx.enter_context(tc.tile_pool(name="keep", bufs=1))
+        hpool = ctx.enter_context(tc.tile_pool(name="hpool", bufs=8))
+        gpool = ctx.enter_context(tc.tile_pool(name="gpool", bufs=4))
+        psum = ctx.enter_context(tc.psum_pool(name="psum", bufs=1))
+        ctx.enter_context(tc.manual_schedule())
+
+        x_sb = keep.tile([P, NT, D_IN], BF16, name="x_sb")
+        mean4 = keep.tile([P, 4], BF16, name="mean4")
+        std4 = keep.tile([P, 4], BF16, name="std4")
+        rstd4 = keep.tile([P, 4], F32, name="rstd4")
+        ident_f = keep.tile([P, P], F32, name="ident_f")
+        ident_b = keep.tile([P, P], BF16, name="ident_b")
+        dvec = keep.tile([P, 1], BF16, name="dvec")
+        rows2 = keep.tile([P, 512], BF16, name="rows2")
+        w1 = keep.tile([P, D_HID], U32, name="w1", align_bytes=64)
+        w2 = keep.tile([P, NG, D_OUT], U32, name="w2", align_bytes=64)
+        w1s = keep.tile([P, 2048], U8, name="w1s", align_bytes=64)
+        w2s = keep.tile([P, 2048], U8, name="w2s", align_bytes=64)
+        bias = keep.tile([P, D_HID], BF16, name="bias")
+        xc = keep.tile([P, NT, 512], F32, name="xc")
+        xg = keep.tile([P, NT, 512], BF16, name="xg", align_bytes=64)
+        xq = keep.tile([P, B], U32, name="xq", align_bytes=64)
+        xqs = keep.tile([P, B], U8, name="xqs", align_bytes=64)
+        hq = keep.tile([P, NG, B], U32, name="hq", align_bytes=64)
+        hqs = keep.tile([P, NG, B], U8, name="hqs", align_bytes=64)
+        warm = keep.tile([P, 1], F32, name="warm")
+        warm2 = keep.tile([P, 1], F32, name="warm2")
+        b2_sb = keep.tile([P, D_OUT], F32, name="b2_sb")
+        os_sb = keep.tile([P, D_OUT], F32, name="os_sb")
+        c_sb = [keep.tile([P, D_OUT], F32, name="c_sb%d" % tt) for tt in range(NT)]
+
+        nc.vector.memset(w1s[:].bitcast(I32), 0)
+        nc.vector.memset(warm[:], 1.0)
+        nc.vector.memset(w2s[:].bitcast(I32), 0)
+        nc.vector.memset(rows2[:], 0.0)
+        make_identity(nc, ident_f[:])
+
+        nc.scalar.dma_start(out=x_sb[:], in_=x.rearrange("(tt p) k -> p tt k", p=P))
+        with nc.allow_non_contiguous_dma(reason="four neighbouring elements to a partition"):
+            nc.scalar.dma_start(out=mean4[:], in_=in_mean.rearrange("(p t) -> p t", t=4))
+            nc.scalar.dma_start(out=std4[:], in_=in_std.rearrange("(p t) -> p t", t=4))
+        nc.scalar.activation(out=warm2[:], in_=warm[:], func=ACT.Sqrt)
+
+        w1_dram = W1_words[0].rearrange("p n t -> p (n t)")
+
+        def load_w1(i):
+            nc.sync.dma_start(out=w1[:, 1024 * i:1024 * (i + 1)].bitcast(I32),
+                              in_=w1_dram[:, 4096 * i:4096 * (i + 1)].bitcast(I32))
+
+        def load_w2(i):
+            nc.sync.dma_start(out=w2[:, 2 * i:2 * i + 2, :].bitcast(I32),
+                              in_=W2_words[2 * i:2 * i + 2].rearrange("g p n t -> p g (n t)").bitcast(I32))
+
+        def load_w1s():
+            for q in range(4):
+                nc.sync.dma_start(
+                    out=w1s[32 * q:32 * q + 16, :].bitcast(I32),
+                    in_=W1_scales[0, 4 * q:4 * q + 4, :].rearrange("r (c n) -> c r n", c=4).bitcast(I32))
+
+        def load_w2s(b):
+            for q in range(4):
+                nc.sync.dma_start(
+                    out=w2s[32 * q:32 * q + 16, 512 * b:512 * (b + 1)].bitcast(I32),
+                    in_=W2_scales[4 * b:4 * b + 4, 4 * q:4 * q + 4, :].bitcast(I32))
+
+        def load_bias(j):
+            nc.sync.dma_start(out=bias[:, 2048 * j:2048 * (j + 1)],
+                              in_=b1[2048 * j:2048 * (j + 1)].partition_broadcast(P))
+
+        def load_rows2():
+            for r, v in enumerate((in_mean, out_mean, out_std, b2)):
+                nc.sync.dma_start(out=rows2[r:r + 1, :], in_=v.unsqueeze(0))
+
+        load_w1(0)
+        load_w1s()
+        load_bias(0)
+        load_rows2()
+        load_w1(1)
+        load_w2s(0)
+        load_w2(0)
+        for j in range(1, 4):
+            load_w1(2 * j)
+            load_w2(2 * j - 1)
+            load_bias(j)
+            load_w1(2 * j + 1)
+            load_w2s(j)
+            load_w2(2 * j)
+        load_w2(7)
+
+        nc.vector.tensor_copy(out=ident_b[:], in_=ident_f[:])
+        nc.vector.tensor_tensor(out=dvec[:], in0=ident_b[:, 1:2], in1=ident_b[:, 0:1], op=ALU.subtract)
+        nc.vector.reciprocal(out=rstd4[:], in_=std4[:])
+
+        xT = psum.tile([P, 2 * NT, P], F32, name="xT", tag="tr0")
+        for tt in range(NT):
+            xw = x_sb[:, tt, :].bitcast(F32)
+            for u in range(2):
+                nc.tensor.transpose(out=xT[:, 2 * tt + u, :], in_=xw[:, u:256:2], identity=ident_f[:])
+        for tt in range(NT):
+            nc.vector.tensor_tensor(
+                out=xc[:, tt, :].rearrange("p (k u e) -> p k u e", u=2, e=2),
+                in0=xT[:, 2 * tt:2 * tt + 2, :].bitcast(BF16).rearrange("p u (k e) -> p k u e", e=2),
+                in1=mean4[:].rearrange("p (u e) -> p u e", e=2).unsqueeze(1).to_broadcast([P, P, 2, 2]),
+                op=ALU.subtract)
+            nc.vector.tensor_tensor(
+                out=xg[:, tt, :].rearrange("p (k t) -> p k t", t=4),
+                in0=xc[:, tt, :].rearrange("p (k t) -> p k t", t=4),
+                in1=rstd4[:].unsqueeze(1).to_broadcast([P, P, 4]),
+                op=ALU.mult)
+            nc.vector.quantize_mx(out=xq[:, P * tt:P * (tt + 1)].bitcast(FP8X4),
+                                  scales=xqs[:, P * tt:P * (tt + 1)], in_=xg[:, tt, :])
+
+        l1_tiles = {}
+        h_tiles = {}
+        tr_tiles = {}
+        hg_tiles = {}
+        acc = []
+
+        def layer1(g, tt):
+            n = 2 * g + tt
+            t = psum.tile([P, 512], F32, name="l1_%d" % n, tag="l1_%d" % (n % 4))
+            l1_tiles[(g, tt)] = t
+            k = 4 * (g // 4)
+            c = 512 * (g % 4)
+            nc.tensor.matmul_mx(out=t[:], lhsT=xq[:, P * tt:P * (tt + 1)].bitcast(FP8X4),
+                                lhsT_scale=xqs[:, P * tt:P * (tt + 1)],
+                                rhs=w1[:, 512 * g:512 * (g + 1)].bitcast(FP8X4),
+                                rhs_scale=w1s[k:P, c:c + 512], start=True, stop=True)
+
+        def add_bias(g, tt):
+            h = hpool.tile([P, 512], BF16, name="h_%d_%d" % (g, tt), tag="h")
+            h_tiles[(g, tt)] = h
+            nc.vector.tensor_tensor(
+                out=h[:].rearrange("p (t j) -> p t j", t=4),
+                in0=l1_tiles[(g, tt)][:].rearrange("p (j t) -> p t j", t=4),
+                in1=bias[:, 512 * g:512 * (g + 1)].rearrange("p (j t) -> p t j", t=4),
+                op=ALU.add)
+
+        def transposes(g):
+            t = psum.tile([P, 4, B], BF16, name="tr_%d" % g, tag="tr%d" % (g % 2))
+            tr_tiles[g] = t
+            for tt in range(NT):
+                for j in range(4):
+                    nc.tensor.transpose(out=t[:, j, P * tt:P * (tt + 1)],
+                                        in_=h_tiles[(g, tt)][:, P * j:P * (j + 1)], identity=ident_b[:])
+
+        def relu(g, engine):
+            hg = gpool.tile([P, 4 * B], BF16, name="hg_%d" % g, tag="hg", align_bytes=64)
+            hg_tiles[g] = hg
+            dst = hg[:].rearrange("p (k t) -> p k t", t=4)
+            src = tr_tiles[g][:].rearrange("p t k -> p k t")
+            if engine == "scalar":
+                nc.scalar.activation(out=dst, in_=src, func=ACT.Relu)
+            else:
+                nc.vector.tensor_scalar_max(out=dst, in0=src, scalar1=0.0)
+
+        def quantise(g):
+            nc.vector.quantize_mx(out=hq[:, g, :].bitcast(FP8X4), scales=hqs[:, g, :], in_=hg_tiles[g][:])
+
+        def layer2(g):
+            k = 4 * (g % 4)
+            c = 512 * (g // 4)
+            for tt in range(NT):
+                nc.tensor.matmul_mx(out=acc[tt][:], lhsT=hq[:, g, P * tt:P * (tt + 1)].bitcast(FP8X4),
+                                    lhsT_scale=hqs[:, g, P * tt:P * (tt + 1)],
+                                    rhs=w2[:, g, :].bitcast(FP8X4), rhs_scale=w2s[k:P, c:c + 512],
+                                    start=(g == 0), stop=(g == NG - 1))
+
+        for g in (0, 1):
+            for tt in range(NT):
+                layer1(g, tt)
+        for g in (0, 1):
+            for tt in range(NT):
+                add_bias(g, tt)
+
+        NS = NG // 2
+        for s in range(NS):
+            nxt = [(g, tt) for g in (2 * s + 2, 2 * s + 3) for tt in range(NT)] if s + 1 < NS else []
+            for g, tt in nxt:
+                layer1(g, tt)
+            if s == 0:
+                ps_b2 = psum.tile([P, 512], F32, name="ps_b2", tag="acc0")
+                nc.tensor.matmul(out=ps_b2[:], lhsT=ident_b[:, 3:4].to_broadcast([P, P]), rhs=rows2[:],
+                                 start=True, stop=True)
+                ps_os = psum.tile([P, 512], F32, name="ps_os", tag="acc1")
+                nc.tensor.matmul(out=ps_os[:], lhsT=ident_b[:, 2:3].to_broadcast([P, P]), rhs=rows2[:],
+                                 start=True, stop=True)
+                nc.scalar.copy(out=b2_sb[:], in_=ps_b2[:])
+                nc.scalar.copy(out=os_sb[:], in_=ps_os[:])
+            if s >= 1:
+                quantise(2 * s - 2)
+            for i, (g, tt) in enumerate(nxt):
+                add_bias(g, tt)
+                if i == 1 and s >= 1:
+                    quantise(2 * s - 1)
+            if not nxt and s >= 1:
+                quantise(2 * s - 1)
+            transposes(2 * s)
+            transposes(2 * s + 1)
+            last = s == NS - 1
+            relu(2 * s, "scalar")
+            relu(2 * s + 1, "vector" if last else "scalar")
+            if s == 0:
+                for tt in range(NT):
+                    ps_c = psum.tile([P, 512], F32, name="ps_c%d" % tt, tag="acc%d" % tt)
+                    nc.tensor.matmul(out=ps_c[:], lhsT=dvec[:, 0:1].to_broadcast([P, P]), rhs=rows2[:],
+                                     start=True, stop=False)
+                    nc.tensor.matmul(out=ps_c[:], lhsT=ident_b[:], rhs=x_sb[:, tt, :], start=False, stop=True)
+                    nc.scalar.copy(out=c_sb[tt][:], in_=ps_c[:])
+            if s == 1:
+                for tt in range(NT):
+                    acc.append(psum.tile([P, 512], F32, name="acc%d" % tt, tag="acc%d" % tt))
+            if s >= 1:
+                layer2(2 * s - 2)
+                layer2(2 * s - 1)
+        quantise(NG - 2)
+        quantise(NG - 1)
+        layer2(NG - 2)
+        layer2(NG - 1)
+
+        nm2 = float(norm_max) * float(norm_max)
+        res, rr, mp, ot, junk = [], [], [], [], []
+        n2, n2c, nr, fac, m2, m2c, mr, rinv = [], [], [], [], [], [], [], []
+        for tt in range(NT):
+            res.append(keep.tile([P, D_OUT], F32, name="res%d" % tt))
+            rr.append(keep.tile([P, D_OUT], F32, name="rr%d" % tt))
+            mp.append(keep.tile([P, D_OUT], F32, name="mp%d" % tt))
+            ot.append(keep.tile([P, D_OUT], F32, name="ot%d" % tt))
+            junk.append(keep.tile([P, D_OUT], F32, name="junk%d" % tt))
+            for lst, nm in ((n2, "n2"), (n2c, "n2c"), (nr, "nr"), (fac, "fac"), (m2, "m2"), (m2c, "m2c"),
+                            (mr, "mr"), (rinv, "rinv")):
+                lst.append(keep.tile([P, 1], F32, name="%s_%d" % (nm, tt)))
+
+        for tt in range(NT):
+            nc.vector.tensor_tensor(out=res[tt][:], in0=acc[tt][:], in1=b2_sb[:], op=ALU.add)
+            nc.scalar.activation(out=junk[tt][:], in_=res[tt][:], func=ACT.Square, accum_out=n2[tt][:])
+        for tt in range(NT):
+            nc.vector.tensor_tensor(out=rr[tt][:], in0=res[tt][:], in1=os_sb[:], op=ALU.mult)
+            nc.vector.tensor_scalar_max(out=n2c[tt][:], in0=n2[tt][:], scalar1=nm2)
+            nc.scalar.activation(out=nr[tt][:], in_=n2c[tt][:], func=ACT.Sqrt, scale=1.0 / nm2)
+        for tt in range(NT):
+            nc.vector.reciprocal(out=fac[tt][:], in_=nr[tt][:])
+            nc.vector.scalar_tensor_tensor(out=mp[tt][:], in0=rr[tt][:], scalar=fac[tt][:, 0:1], in1=c_sb[tt][:],
+                                           op0=ALU.mult, op1=ALU.add)
+            nc.scalar.activation(out=junk[tt][:], in_=mp[tt][:], func=ACT.Square, accum_out=m2[tt][:])
+        for tt in range(NT):
+            nc.vector.tensor_scalar_max(out=m2c[tt][:], in0=m2[tt][:], scalar1=EPS * EPS)
+            nc.scalar.activation(out=mr[tt][:], in_=m2c[tt][:], func=ACT.Sqrt)
+        for tt in range(NT):
+            nc.vector.reciprocal(out=rinv[tt][:], in_=mr[tt][:])
+            if tt == 0:
+                nc.scalar.activation(out=ot[tt][:], in_=mp[tt][:], func=ACT.Copy, scale=rinv[tt][:, 0:1])
+            else:
+                nc.vector.tensor_scalar_mul(out=ot[tt][:], in0=mp[tt][:], scalar1=rinv[tt][:, 0:1])
+            nc.sync.dma_start(out=out[P * tt:P * (tt + 1), :], in_=ot[tt][:])

@@ -40,6 +40,7 @@ def tile_mlp_w_kernel(tc, x, in_mean, in_std, out_mean, out_std, W1_words, W1_sc
         ident_b = keep.tile([P, P], BF16, name="ident_b")
         dvec = keep.tile([P, 1], BF16, name="dvec")
         rows2 = keep.tile([P, 512], BF16, name="rows2")
+        rows1 = keep.tile([P, 512], BF16, name="rows1")
         w1 = keep.tile([P, D_HID], U32, name="w1", align_bytes=64)
         w2 = keep.tile([P, NG, D_OUT], U32, name="w2", align_bytes=64)
         w1s = keep.tile([P, 2048], U8, name="w1s", align_bytes=64)
@@ -54,9 +55,8 @@ def tile_mlp_w_kernel(tc, x, in_mean, in_std, out_mean, out_std, W1_words, W1_sc
         warm = keep.tile([P, 1], F32, name="warm")
         warm2 = keep.tile([P, 1], F32, name="warm2")
         b2_sb = keep.tile([P, D_OUT], F32, name="b2_sb")
-        os_sb = keep.tile([P, D_OUT], F32, name="os_sb")
-        c_sb = [keep.tile([P, D_OUT], F32, name="c_sb%d" % tt) for tt in range(NT)]
 
+        nc.vector.memset(rows1[:], 0.0)
         nc.vector.memset(w1s[:].bitcast(I32), 0)
         nc.vector.memset(warm[:], 1.0)
         nc.vector.memset(w2s[:].bitcast(I32), 0)
@@ -67,6 +67,7 @@ def tile_mlp_w_kernel(tc, x, in_mean, in_std, out_mean, out_std, W1_words, W1_sc
         with nc.allow_non_contiguous_dma(reason="four neighbouring elements to a partition"):
             nc.scalar.dma_start(out=mean4[:], in_=in_mean.rearrange("(p t) -> p t", t=4))
             nc.scalar.dma_start(out=std4[:], in_=in_std.rearrange("(p t) -> p t", t=4))
+        nc.scalar.dma_start(out=rows1[0:NG, :], in_=b1.rearrange("(g n) -> g n", g=NG))
         nc.scalar.activation(out=warm2[:], in_=warm[:], func=ACT.Sqrt)
 
         w1_dram = W1_words[0].rearrange("p n t -> p (n t)")
@@ -91,17 +92,12 @@ def tile_mlp_w_kernel(tc, x, in_mean, in_std, out_mean, out_std, W1_words, W1_sc
                     out=w2s[32 * q:32 * q + 16, 512 * b:512 * (b + 1)].bitcast(I32),
                     in_=W2_scales[4 * b:4 * b + 4, 4 * q:4 * q + 4, :].bitcast(I32))
 
-        def load_bias(j):
-            nc.sync.dma_start(out=bias[:, 2048 * j:2048 * (j + 1)],
-                              in_=b1[2048 * j:2048 * (j + 1)].partition_broadcast(P))
-
         def load_rows2():
             for r, v in enumerate((in_mean, out_mean, out_std, b2)):
                 nc.sync.dma_start(out=rows2[r:r + 1, :], in_=v.unsqueeze(0))
 
         load_w1(0)
         load_w1s()
-        load_bias(0)
         load_rows2()
         load_w1(1)
         load_w2s(0)
@@ -109,7 +105,6 @@ def tile_mlp_w_kernel(tc, x, in_mean, in_std, out_mean, out_std, W1_words, W1_sc
         for j in range(1, 4):
             load_w1(2 * j)
             load_w2(2 * j - 1)
-            load_bias(j)
             load_w1(2 * j + 1)
             load_w2s(j)
             load_w2(2 * j)
@@ -119,11 +114,21 @@ def tile_mlp_w_kernel(tc, x, in_mean, in_std, out_mean, out_std, W1_words, W1_sc
         nc.vector.tensor_tensor(out=dvec[:], in0=ident_b[:, 1:2], in1=ident_b[:, 0:1], op=ALU.subtract)
         nc.vector.reciprocal(out=rstd4[:], in_=std4[:])
 
+        def spread_bias(i, tag):
+            bp = psum.tile([P, 1024], BF16, name="bp%d" % i, tag=tag)
+            for hh in range(2):
+                g = 2 * i + hh
+                nc.tensor.matmul(out=bp[:, 512 * hh:512 * (hh + 1)], lhsT=ident_b[:, g:g + 1].to_broadcast([P, P]),
+                                 rhs=rows1[:], start=True, stop=True)
+            nc.scalar.copy(out=bias[:, 1024 * i:1024 * (i + 1)], in_=bp[:])
+
         xT = psum.tile([P, 2 * NT, P], F32, name="xT", tag="tr0")
         for tt in range(NT):
             xw = x_sb[:, tt, :].bitcast(F32)
             for u in range(2):
                 nc.tensor.transpose(out=xT[:, 2 * tt + u, :], in_=xw[:, u:256:2], identity=ident_f[:])
+        spread_bias(0, "acc0")
+        spread_bias(1, "acc1")
         for tt in range(NT):
             nc.vector.tensor_tensor(
                 out=xc[:, tt, :].rearrange("p (k u e) -> p k u e", u=2, e=2),
@@ -143,6 +148,7 @@ def tile_mlp_w_kernel(tc, x, in_mean, in_std, out_mean, out_std, W1_words, W1_sc
         tr_tiles = {}
         hg_tiles = {}
         acc = []
+        ps_c = []
 
         def layer1(g, tt):
             n = 2 * g + tt
@@ -197,6 +203,8 @@ def tile_mlp_w_kernel(tc, x, in_mean, in_std, out_mean, out_std, W1_words, W1_sc
         for g in (0, 1):
             for tt in range(NT):
                 layer1(g, tt)
+        spread_bias(2, "tr1")
+        spread_bias(3, "acc0")
         for g in (0, 1):
             for tt in range(NT):
                 add_bias(g, tt)
@@ -207,14 +215,8 @@ def tile_mlp_w_kernel(tc, x, in_mean, in_std, out_mean, out_std, W1_words, W1_sc
             for g, tt in nxt:
                 layer1(g, tt)
             if s == 0:
-                ps_b2 = psum.tile([P, 512], F32, name="ps_b2", tag="acc0")
-                nc.tensor.matmul(out=ps_b2[:], lhsT=ident_b[:, 3:4].to_broadcast([P, P]), rhs=rows2[:],
-                                 start=True, stop=True)
-                ps_os = psum.tile([P, 512], F32, name="ps_os", tag="acc1")
-                nc.tensor.matmul(out=ps_os[:], lhsT=ident_b[:, 2:3].to_broadcast([P, P]), rhs=rows2[:],
-                                 start=True, stop=True)
-                nc.scalar.copy(out=b2_sb[:], in_=ps_b2[:])
-                nc.scalar.copy(out=os_sb[:], in_=ps_os[:])
+                spread_bias(4, "acc1")
+                spread_bias(5, "acc0")
             if s >= 1:
                 quantise(2 * s - 2)
             for i, (g, tt) in enumerate(nxt):
@@ -229,12 +231,21 @@ def tile_mlp_w_kernel(tc, x, in_mean, in_std, out_mean, out_std, W1_words, W1_sc
             relu(2 * s, "scalar")
             relu(2 * s + 1, "vector" if last else "scalar")
             if s == 0:
+                spread_bias(6, "acc1")
+                spread_bias(7, "acc0")
+            if last:
+                ps_b2 = psum.tile([P, 512], F32, name="ps_b2", tag="l1_0")
+                nc.tensor.matmul(out=ps_b2[:], lhsT=ident_b[:, 3:4].to_broadcast([P, P]), rhs=rows2[:],
+                                 start=True, stop=True)
+                nc.scalar.copy(out=b2_sb[:], in_=ps_b2[:])
+                ps_os = psum.tile([P, 512], F32, name="ps_os", tag="l1_1")
+                nc.tensor.matmul(out=ps_os[:], lhsT=ident_b[:, 2:3].to_broadcast([P, P]), rhs=rows2[:],
+                                 start=True, stop=True)
                 for tt in range(NT):
-                    ps_c = psum.tile([P, 512], F32, name="ps_c%d" % tt, tag="acc%d" % tt)
-                    nc.tensor.matmul(out=ps_c[:], lhsT=dvec[:, 0:1].to_broadcast([P, P]), rhs=rows2[:],
+                    ps_c.append(psum.tile([P, 512], F32, name="ps_c%d" % tt, tag="l1_%d" % (2 + tt)))
+                    nc.tensor.matmul(out=ps_c[tt][:], lhsT=dvec[:, 0:1].to_broadcast([P, P]), rhs=rows2[:],
                                      start=True, stop=False)
-                    nc.tensor.matmul(out=ps_c[:], lhsT=ident_b[:], rhs=x_sb[:, tt, :], start=False, stop=True)
-                    nc.scalar.copy(out=c_sb[tt][:], in_=ps_c[:])
+                    nc.tensor.matmul(out=ps_c[tt][:], lhsT=ident_b[:], rhs=x_sb[:, tt, :], start=False, stop=True)
             if s == 1:
                 for tt in range(NT):
                     acc.append(psum.tile([P, 512], F32, name="acc%d" % tt, tag="acc%d" % tt))
@@ -263,12 +274,12 @@ def tile_mlp_w_kernel(tc, x, in_mean, in_std, out_mean, out_std, W1_words, W1_sc
             nc.vector.tensor_tensor(out=res[tt][:], in0=acc[tt][:], in1=b2_sb[:], op=ALU.add)
             nc.scalar.activation(out=junk[tt][:], in_=res[tt][:], func=ACT.Square, accum_out=n2[tt][:])
         for tt in range(NT):
-            nc.vector.tensor_tensor(out=rr[tt][:], in0=res[tt][:], in1=os_sb[:], op=ALU.mult)
+            nc.vector.tensor_tensor(out=rr[tt][:], in0=res[tt][:], in1=ps_os[:], op=ALU.mult)
             nc.vector.tensor_scalar_max(out=n2c[tt][:], in0=n2[tt][:], scalar1=nm2)
             nc.scalar.activation(out=nr[tt][:], in_=n2c[tt][:], func=ACT.Sqrt, scale=1.0 / nm2)
         for tt in range(NT):
             nc.vector.reciprocal(out=fac[tt][:], in_=nr[tt][:])
-            nc.vector.scalar_tensor_tensor(out=mp[tt][:], in0=rr[tt][:], scalar=fac[tt][:, 0:1], in1=c_sb[tt][:],
+            nc.vector.scalar_tensor_tensor(out=mp[tt][:], in0=rr[tt][:], scalar=fac[tt][:, 0:1], in1=ps_c[tt][:],
                                            op0=ALU.mult, op1=ALU.add)
             nc.scalar.activation(out=junk[tt][:], in_=mp[tt][:], func=ACT.Square, accum_out=m2[tt][:])
         for tt in range(NT):

@@ -55,6 +55,9 @@ def tile_mlp_w_kernel(tc, x, in_mean, in_std, out_mean, out_std, W1_words, W1_sc
         warm = keep.tile([P, 1], F32, name="warm")
         warm2 = keep.tile([P, 1], F32, name="warm2")
         b2_sb = keep.tile([P, D_OUT], F32, name="b2_sb")
+        os_sb = keep.tile([P, D_OUT], F32, name="os_sb")
+        d_sb = keep.tile([P, D_OUT], F32, name="d_sb")
+        c_sb = [keep.tile([P, D_OUT], F32, name="c_sb%d" % tt) for tt in range(NT)]
 
         nc.vector.memset(rows1[:], 0.0)
         nc.vector.memset(w1s[:].bitcast(I32), 0)
@@ -62,13 +65,14 @@ def tile_mlp_w_kernel(tc, x, in_mean, in_std, out_mean, out_std, W1_words, W1_sc
         nc.vector.memset(w2s[:].bitcast(I32), 0)
         nc.vector.memset(rows2[:], 0.0)
         make_identity(nc, ident_f[:])
+        make_identity(nc, ident_b[:])
 
         nc.scalar.dma_start(out=x_sb[:], in_=x.rearrange("(tt p) k -> p tt k", p=P))
         with nc.allow_non_contiguous_dma(reason="four neighbouring elements to a partition"):
             nc.scalar.dma_start(out=mean4[:], in_=in_mean.rearrange("(p t) -> p t", t=4))
             nc.scalar.dma_start(out=std4[:], in_=in_std.rearrange("(p t) -> p t", t=4))
         nc.scalar.dma_start(out=rows1[0:NG, :], in_=b1.rearrange("(g n) -> g n", g=NG))
-        nc.scalar.activation(out=warm2[:], in_=warm[:], func=ACT.Sqrt)
+        nc.scalar.activation(out=warm2[:], in_=warm[:], func=ACT.Abs_reciprocal_sqrt)
 
         w1_dram = W1_words[0].rearrange("p n t -> p (n t)")
 
@@ -110,7 +114,6 @@ def tile_mlp_w_kernel(tc, x, in_mean, in_std, out_mean, out_std, W1_words, W1_sc
             load_w2(2 * j)
         load_w2(7)
 
-        nc.vector.tensor_copy(out=ident_b[:], in_=ident_f[:])
         nc.vector.tensor_tensor(out=dvec[:], in0=ident_b[:, 1:2], in1=ident_b[:, 0:1], op=ALU.subtract)
         nc.vector.reciprocal(out=rstd4[:], in_=std4[:])
 
@@ -129,6 +132,8 @@ def tile_mlp_w_kernel(tc, x, in_mean, in_std, out_mean, out_std, W1_words, W1_sc
                 nc.tensor.transpose(out=xT[:, 2 * tt + u, :], in_=xw[:, u:256:2], identity=ident_f[:])
         spread_bias(0, "acc0")
         spread_bias(1, "acc1")
+        spread_bias(2, "tr1")
+        spread_bias(3, "acc0")
         for tt in range(NT):
             nc.vector.tensor_tensor(
                 out=xc[:, tt, :].rearrange("p (k u e) -> p k u e", u=2, e=2),
@@ -148,7 +153,6 @@ def tile_mlp_w_kernel(tc, x, in_mean, in_std, out_mean, out_std, W1_words, W1_sc
         tr_tiles = {}
         hg_tiles = {}
         acc = []
-        ps_c = []
 
         def layer1(g, tt):
             n = 2 * g + tt
@@ -191,104 +195,128 @@ def tile_mlp_w_kernel(tc, x, in_mean, in_std, out_mean, out_std, W1_words, W1_sc
         def quantise(g):
             nc.vector.quantize_mx(out=hq[:, g, :].bitcast(FP8X4), scales=hqs[:, g, :], in_=hg_tiles[g][:])
 
-        def layer2(g):
+        def layer2(g, tiles):
             k = 4 * (g % 4)
             c = 512 * (g // 4)
-            for tt in range(NT):
+            for tt in tiles:
                 nc.tensor.matmul_mx(out=acc[tt][:], lhsT=hq[:, g, P * tt:P * (tt + 1)].bitcast(FP8X4),
                                     lhsT_scale=hqs[:, g, P * tt:P * (tt + 1)],
                                     rhs=w2[:, g, :].bitcast(FP8X4), rhs_scale=w2s[k:P, c:c + 512],
                                     start=(g == 0), stop=(g == NG - 1))
 
+        def spread_row(sel, dst, tag):
+            ps = psum.tile([P, 512], F32, name="ps_" + tag, tag=tag)
+            nc.tensor.matmul(out=ps[:], lhsT=sel.to_broadcast([P, P]), rhs=rows2[:], start=True, stop=True)
+            nc.scalar.copy(out=dst[:], in_=ps[:])
+
         for g in (0, 1):
             for tt in range(NT):
                 layer1(g, tt)
-        spread_bias(2, "tr1")
-        spread_bias(3, "acc0")
+        spread_bias(4, "acc1")
+        spread_bias(5, "tr1")
         for g in (0, 1):
+            for tt in range(NT):
+                add_bias(g, tt)
+        for g in (2, 3):
+            for tt in range(NT):
+                layer1(g, tt)
+        spread_bias(6, "acc0")
+        spread_bias(7, "acc1")
+        spread_row(ident_b[:, 3:4], b2_sb, "tr1")
+        spread_row(ident_b[:, 2:3], os_sb, "acc0")
+        spread_row(dvec[:, 0:1], d_sb, "acc1")
+        for tt in range(NT):
+            nc.gpsimd.tensor_tensor(out=c_sb[tt][:], in0=x_sb[:, tt, :], in1=d_sb[:], op=ALU.add)
+        for g in (2, 3):
             for tt in range(NT):
                 add_bias(g, tt)
 
         NS = NG // 2
+        POST_FROM = 4
+        FILL = 4
+        post = []
         for s in range(NS):
-            nxt = [(g, tt) for g in (2 * s + 2, 2 * s + 3) for tt in range(NT)] if s + 1 < NS else []
+            nxt = [(g, tt) for g in (2 * s + 2, 2 * s + 3) for tt in range(NT)] if 1 <= s < NS - 1 else []
             for g, tt in nxt:
                 layer1(g, tt)
-            if s == 0:
-                spread_bias(4, "acc1")
-                spread_bias(5, "acc0")
             if s >= 1:
                 quantise(2 * s - 2)
             for i, (g, tt) in enumerate(nxt):
                 add_bias(g, tt)
-                if i == 1 and s >= 1:
+                if i == 1:
                     quantise(2 * s - 1)
             if not nxt and s >= 1:
                 quantise(2 * s - 1)
             transposes(2 * s)
             transposes(2 * s + 1)
-            last = s == NS - 1
             relu(2 * s, "scalar")
-            relu(2 * s + 1, "vector" if last else "scalar")
-            if s == 0:
-                spread_bias(6, "acc1")
-                spread_bias(7, "acc0")
-            if last:
-                ps_b2 = psum.tile([P, 512], F32, name="ps_b2", tag="l1_0")
-                nc.tensor.matmul(out=ps_b2[:], lhsT=ident_b[:, 3:4].to_broadcast([P, P]), rhs=rows2[:],
-                                 start=True, stop=True)
-                nc.scalar.copy(out=b2_sb[:], in_=ps_b2[:])
-                ps_os = psum.tile([P, 512], F32, name="ps_os", tag="l1_1")
-                nc.tensor.matmul(out=ps_os[:], lhsT=ident_b[:, 2:3].to_broadcast([P, P]), rhs=rows2[:],
-                                 start=True, stop=True)
-                for tt in range(NT):
-                    ps_c.append(psum.tile([P, 512], F32, name="ps_c%d" % tt, tag="l1_%d" % (2 + tt)))
-                    nc.tensor.matmul(out=ps_c[tt][:], lhsT=dvec[:, 0:1].to_broadcast([P, P]), rhs=rows2[:],
-                                     start=True, stop=False)
-                    nc.tensor.matmul(out=ps_c[tt][:], lhsT=ident_b[:], rhs=x_sb[:, tt, :], start=False, stop=True)
+            relu(2 * s + 1, "vector" if s == NS - 1 else "scalar")
             if s == 1:
                 for tt in range(NT):
                     acc.append(psum.tile([P, 512], F32, name="acc%d" % tt, tag="acc%d" % tt))
             if s >= 1:
-                layer2(2 * s - 2)
-                layer2(2 * s - 1)
+                for g in (2 * s - 2, 2 * s - 1):
+                    if g >= POST_FROM:
+                        layer2(g, (0,))
+                        post.append(g)
+                    else:
+                        layer2(g, (0, 1))
         quantise(NG - 2)
         quantise(NG - 1)
-        layer2(NG - 2)
-        layer2(NG - 1)
+        for g in post[:FILL]:
+            layer2(g, (1,))
+        layer2(NG - 2, (0,))
+        layer2(NG - 1, (0,))
+        for g in post[FILL:]:
+            layer2(g, (1,))
+        layer2(NG - 2, (1,))
+        layer2(NG - 1, (1,))
 
         nm2 = float(norm_max) * float(norm_max)
         res, rr, mp, ot, junk = [], [], [], [], []
-        n2, n2c, nr, fac, m2, m2c, mr, rinv = [], [], [], [], [], [], [], []
+        n2, f0, fac, m2, r0, rinv = [], [], [], [], [], []
         for tt in range(NT):
             res.append(keep.tile([P, D_OUT], F32, name="res%d" % tt))
             rr.append(keep.tile([P, D_OUT], F32, name="rr%d" % tt))
             mp.append(keep.tile([P, D_OUT], F32, name="mp%d" % tt))
             ot.append(keep.tile([P, D_OUT], F32, name="ot%d" % tt))
             junk.append(keep.tile([P, D_OUT], F32, name="junk%d" % tt))
-            for lst, nm in ((n2, "n2"), (n2c, "n2c"), (nr, "nr"), (fac, "fac"), (m2, "m2"), (m2c, "m2c"),
-                            (mr, "mr"), (rinv, "rinv")):
+            for lst, nm in ((n2, "n2"), (f0, "f0"), (fac, "fac"), (m2, "m2"), (r0, "r0"), (rinv, "rinv")):
                 lst.append(keep.tile([P, 1], F32, name="%s_%d" % (nm, tt)))
 
-        for tt in range(NT):
+        def end_add(tt):
             nc.vector.tensor_tensor(out=res[tt][:], in0=acc[tt][:], in1=b2_sb[:], op=ALU.add)
+
+        def end_norm1(tt):
             nc.scalar.activation(out=junk[tt][:], in_=res[tt][:], func=ACT.Square, accum_out=n2[tt][:])
-        for tt in range(NT):
-            nc.vector.tensor_tensor(out=rr[tt][:], in0=res[tt][:], in1=ps_os[:], op=ALU.mult)
-            nc.vector.tensor_scalar_max(out=n2c[tt][:], in0=n2[tt][:], scalar1=nm2)
-            nc.scalar.activation(out=nr[tt][:], in_=n2c[tt][:], func=ACT.Sqrt, scale=1.0 / nm2)
-        for tt in range(NT):
-            nc.vector.reciprocal(out=fac[tt][:], in_=nr[tt][:])
-            nc.vector.scalar_tensor_tensor(out=mp[tt][:], in0=rr[tt][:], scalar=fac[tt][:, 0:1], in1=ps_c[tt][:],
+            nc.scalar.activation(out=f0[tt][:], in_=n2[tt][:], func=ACT.Abs_reciprocal_sqrt, scale=1.0 / nm2)
+
+        def end_gain(tt):
+            nc.vector.tensor_tensor(out=rr[tt][:], in0=res[tt][:], in1=os_sb[:], op=ALU.mult)
+
+        def end_map(tt):
+            nc.vector.tensor_scalar_min(out=fac[tt][:], in0=f0[tt][:], scalar1=1.0)
+            nc.vector.scalar_tensor_tensor(out=mp[tt][:], in0=rr[tt][:], scalar=fac[tt][:, 0:1], in1=c_sb[tt][:],
                                            op0=ALU.mult, op1=ALU.add)
+
+        def end_norm2(tt):
             nc.scalar.activation(out=junk[tt][:], in_=mp[tt][:], func=ACT.Square, accum_out=m2[tt][:])
-        for tt in range(NT):
-            nc.vector.tensor_scalar_max(out=m2c[tt][:], in0=m2[tt][:], scalar1=EPS * EPS)
-            nc.scalar.activation(out=mr[tt][:], in_=m2c[tt][:], func=ACT.Sqrt)
-        for tt in range(NT):
-            nc.vector.reciprocal(out=rinv[tt][:], in_=mr[tt][:])
-            if tt == 0:
-                nc.scalar.activation(out=ot[tt][:], in_=mp[tt][:], func=ACT.Copy, scale=rinv[tt][:, 0:1])
-            else:
-                nc.vector.tensor_scalar_mul(out=ot[tt][:], in0=mp[tt][:], scalar1=rinv[tt][:, 0:1])
+            nc.scalar.activation(out=r0[tt][:], in_=m2[tt][:], func=ACT.Abs_reciprocal_sqrt)
+
+        def end_out(tt):
+            nc.vector.tensor_scalar_min(out=rinv[tt][:], in0=r0[tt][:], scalar1=1.0 / EPS)
+            nc.vector.tensor_scalar_mul(out=ot[tt][:], in0=mp[tt][:], scalar1=rinv[tt][:, 0:1])
             nc.sync.dma_start(out=out[P * tt:P * (tt + 1), :], in_=ot[tt][:])
+
+        end_add(0)
+        end_norm1(0)
+        end_gain(0)
+        end_map(0)
+        end_add(1)
+        end_norm2(0)
+        end_gain(1)
+        end_out(0)
+        end_norm1(1)
+        end_map(1)
+        end_norm2(1)
+        end_out(1)

@@ -28,7 +28,7 @@ def tile_mlp_w_kernel(tc, x, in_mean, in_std, out_mean, out_std, W1_words, W1_sc
     with ExitStack() as ctx:
         keep = ctx.enter_context(tc.tile_pool(name="keep", bufs=1))
         hpool = ctx.enter_context(tc.tile_pool(name="hpool", bufs=8))
-        gpool = ctx.enter_context(tc.tile_pool(name="gpool", bufs=4))
+        gpool = ctx.enter_context(tc.tile_pool(name="gpool", bufs=6))
         psum = ctx.enter_context(tc.psum_pool(name="psum", bufs=1))
         ctx.enter_context(tc.manual_schedule())
 
@@ -56,7 +56,6 @@ def tile_mlp_w_kernel(tc, x, in_mean, in_std, out_mean, out_std, W1_words, W1_sc
         warm2 = keep.tile([P, 1], F32, name="warm2")
         b2_sb = keep.tile([P, D_OUT], F32, name="b2_sb")
         os_sb = keep.tile([P, D_OUT], F32, name="os_sb")
-        d_sb = keep.tile([P, D_OUT], F32, name="d_sb")
         c_sb = [keep.tile([P, D_OUT], F32, name="c_sb%d" % tt) for tt in range(NT)]
 
         nc.vector.memset(rows1[:], 0.0)
@@ -224,51 +223,40 @@ def tile_mlp_w_kernel(tc, x, in_mean, in_std, out_mean, out_std, W1_words, W1_sc
         spread_bias(7, "acc1")
         spread_row(ident_b[:, 3:4], b2_sb, "tr1")
         spread_row(ident_b[:, 2:3], os_sb, "acc0")
-        spread_row(dvec[:, 0:1], d_sb, "acc1")
-        for tt in range(NT):
-            nc.gpsimd.tensor_tensor(out=c_sb[tt][:], in0=x_sb[:, tt, :], in1=d_sb[:], op=ALU.add)
+        ps_d = psum.tile([P, 512], F32, name="ps_d", tag="acc1")
+        nc.tensor.matmul(out=ps_d[:], lhsT=dvec[:, 0:1].to_broadcast([P, P]), rhs=rows2[:], start=True, stop=True)
         for g in (2, 3):
             for tt in range(NT):
                 add_bias(g, tt)
+        for tt in range(NT):
+            nc.vector.tensor_tensor(out=c_sb[tt][:], in0=ps_d[:], in1=x_sb[:, tt, :], op=ALU.add)
 
         NS = NG // 2
-        POST_FROM = 4
-        FILL = 4
-        post = []
         for s in range(NS):
             nxt = [(g, tt) for g in (2 * s + 2, 2 * s + 3) for tt in range(NT)] if 1 <= s < NS - 1 else []
             for g, tt in nxt:
                 layer1(g, tt)
+            for g, tt in nxt:
+                add_bias(g, tt)
             if s >= 1:
                 quantise(2 * s - 2)
-            for i, (g, tt) in enumerate(nxt):
-                add_bias(g, tt)
-                if i == 1:
-                    quantise(2 * s - 1)
-            if not nxt and s >= 1:
                 quantise(2 * s - 1)
             transposes(2 * s)
             transposes(2 * s + 1)
             relu(2 * s, "scalar")
             relu(2 * s + 1, "vector" if s == NS - 1 else "scalar")
-            if s == 1:
+            if s == 2:
                 for tt in range(NT):
                     acc.append(psum.tile([P, 512], F32, name="acc%d" % tt, tag="acc%d" % tt))
-            if s >= 1:
-                for g in (2 * s - 2, 2 * s - 1):
-                    if g >= POST_FROM:
-                        layer2(g, (0,))
-                        post.append(g)
-                    else:
-                        layer2(g, (0, 1))
+            if s >= 2:
+                layer2(2 * s - 4, (0, 1))
+                layer2(2 * s - 3, (0, 1))
+        layer2(NG - 4, (0, 1))
+        layer2(NG - 3, (0, 1))
         quantise(NG - 2)
         quantise(NG - 1)
-        for g in post[:FILL]:
-            layer2(g, (1,))
         layer2(NG - 2, (0,))
         layer2(NG - 1, (0,))
-        for g in post[FILL:]:
-            layer2(g, (1,))
         layer2(NG - 2, (1,))
         layer2(NG - 1, (1,))
 
@@ -308,15 +296,6 @@ def tile_mlp_w_kernel(tc, x, in_mean, in_std, out_mean, out_std, W1_words, W1_sc
             nc.vector.tensor_scalar_mul(out=ot[tt][:], in0=mp[tt][:], scalar1=rinv[tt][:, 0:1])
             nc.sync.dma_start(out=out[P * tt:P * (tt + 1), :], in_=ot[tt][:])
 
-        end_add(0)
-        end_norm1(0)
-        end_gain(0)
-        end_map(0)
-        end_add(1)
-        end_norm2(0)
-        end_gain(1)
-        end_out(0)
-        end_norm1(1)
-        end_map(1)
-        end_norm2(1)
-        end_out(1)
+        for stage in (end_add, end_norm1, end_gain, end_map, end_norm2, end_out):
+            for tt in range(NT):
+                stage(tt)

@@ -103,14 +103,24 @@ def tile_mlp_w_kernel(tc, x, in_mean, in_std, out_mean, out_std, W1_words, W1_sc
         load_w1s()
         load_rows2()
         load_w1(1)
+        load_w1(2)
         load_w2s(0)
         load_w2(0)
-        for j in range(1, 4):
-            load_w1(2 * j)
-            load_w2(2 * j - 1)
-            load_w1(2 * j + 1)
-            load_w2s(j)
-            load_w2(2 * j)
+        load_w1(3)
+        load_w2(1)
+        load_w1(4)
+        load_w2s(1)
+        load_w2(2)
+        load_w1(5)
+        nc.sync.dma_start(out=bias[:, 6144:8192], in_=b1[6144:8192].partition_broadcast(P))
+        load_w1(6)
+        load_w2(3)
+        load_w2s(2)
+        load_w1(7)
+        load_w2(4)
+        load_w2(5)
+        load_w2s(3)
+        load_w2(6)
         load_w2(7)
 
         nc.vector.tensor_tensor(out=dvec[:], in0=ident_b[:, 1:2], in1=ident_b[:, 0:1], op=ALU.subtract)
@@ -219,8 +229,6 @@ def tile_mlp_w_kernel(tc, x, in_mean, in_std, out_mean, out_std, W1_words, W1_sc
         for g in (2, 3):
             for tt in range(NT):
                 layer1(g, tt)
-        spread_bias(6, "acc0")
-        spread_bias(7, "acc1")
         spread_row(ident_b[:, 3:4], b2_sb, "tr1")
         spread_row(ident_b[:, 2:3], os_sb, "acc0")
         ps_d = psum.tile([P, 512], F32, name="ps_d", tag="acc1")

@@ -104,14 +104,15 @@ def tile_mlp_w_kernel(tc, x, in_mean, in_std, out_mean, out_std, W1_words, W1_sc
         load_rows2()
         load_w1(1)
         load_w1(2)
+        load_w1(3)
+        nc.sync.dma_start(out=bias[:, 4096:6144], in_=b1[4096:6144].partition_broadcast(P))
         load_w2s(0)
         load_w2(0)
-        load_w1(3)
-        load_w2(1)
         load_w1(4)
+        load_w2(1)
+        load_w1(5)
         load_w2s(1)
         load_w2(2)
-        load_w1(5)
         nc.sync.dma_start(out=bias[:, 6144:8192], in_=b1[6144:8192].partition_broadcast(P))
         load_w1(6)
         load_w2(3)
@@ -221,8 +222,6 @@ def tile_mlp_w_kernel(tc, x, in_mean, in_std, out_mean, out_std, W1_words, W1_sc
         for g in (0, 1):
             for tt in range(NT):
                 layer1(g, tt)
-        spread_bias(4, "acc1")
-        spread_bias(5, "tr1")
         for g in (0, 1):
             for tt in range(NT):
                 add_bias(g, tt)

@@ -1,8 +1,6 @@
 from contextlib import ExitStack
 
-import concourse.bass as bass
 import concourse.mybir as mybir
-import concourse.tile as tile
 from concourse.masks import make_identity
 
 F32 = mybir.dt.float32
@@ -20,6 +18,8 @@ NT = B // P
 NG = D_HID // 512
 EPS = 1e-12
 FLOPS = 2 * B * D_IN * D_HID + 2 * B * D_HID * D_OUT
+LEAD = 2
+LAG = 3
 
 
 def tile_mlp_w_kernel(tc, x, in_mean, in_std, out_mean, out_std, W1_words, W1_scales, b1,
@@ -27,8 +27,8 @@ def tile_mlp_w_kernel(tc, x, in_mean, in_std, out_mean, out_std, W1_words, W1_sc
     nc = tc.nc
     with ExitStack() as ctx:
         keep = ctx.enter_context(tc.tile_pool(name="keep", bufs=1))
-        hpool = ctx.enter_context(tc.tile_pool(name="hpool", bufs=8))
-        gpool = ctx.enter_context(tc.tile_pool(name="gpool", bufs=6))
+        spool = ctx.enter_context(tc.tile_pool(name="spool", bufs=3))
+        gpool = ctx.enter_context(tc.tile_pool(name="gpool", bufs=3))
         psum = ctx.enter_context(tc.psum_pool(name="psum", bufs=1))
         ctx.enter_context(tc.manual_schedule())
 
@@ -40,14 +40,16 @@ def tile_mlp_w_kernel(tc, x, in_mean, in_std, out_mean, out_std, W1_words, W1_sc
         ident_b = keep.tile([P, P], BF16, name="ident_b")
         dvec = keep.tile([P, 1], BF16, name="dvec")
         rows2 = keep.tile([P, 512], BF16, name="rows2")
-        rows1 = keep.tile([P, 512], BF16, name="rows1")
-        w1 = keep.tile([P, D_HID], U32, name="w1", align_bytes=64)
+        w1r = keep.tile([P, D_HID], U32, name="w1r", align_bytes=64)
+        w1p = keep.tile([P, D_HID], U32, name="w1p", align_bytes=64)
         w2 = keep.tile([P, NG, D_OUT], U32, name="w2", align_bytes=64)
-        w1s = keep.tile([P, 2048], U8, name="w1s", align_bytes=64)
+        w1sr = keep.tile([P, 2048], U8, name="w1sr", align_bytes=64)
+        w1sp = keep.tile([P, 2048], U8, name="w1sp", align_bytes=64)
         w2s = keep.tile([P, 2048], U8, name="w2s", align_bytes=64)
-        bias = keep.tile([P, D_HID], BF16, name="bias")
+        b1t = keep.tile([P, NG, 4], BF16, name="b1t")
+        b1f = keep.tile([P, NG * 4], F32, name="b1f")
         xc = keep.tile([P, NT, 512], F32, name="xc")
-        xg = keep.tile([P, NT, 512], BF16, name="xg", align_bytes=64)
+        xg = keep.tile([P, NT * 512], BF16, name="xg", align_bytes=64)
         xq = keep.tile([P, B], U32, name="xq", align_bytes=64)
         xqs = keep.tile([P, B], U8, name="xqs", align_bytes=64)
         hq = keep.tile([P, NG, B], U32, name="hq", align_bytes=64)
@@ -58,11 +60,10 @@ def tile_mlp_w_kernel(tc, x, in_mean, in_std, out_mean, out_std, W1_words, W1_sc
         os_sb = keep.tile([P, D_OUT], F32, name="os_sb")
         c_sb = [keep.tile([P, D_OUT], F32, name="c_sb%d" % tt) for tt in range(NT)]
 
-        nc.vector.memset(rows1[:], 0.0)
-        nc.vector.memset(w1s[:].bitcast(I32), 0)
+        nc.vector.memset(w1sr[:].bitcast(I32), 0)
+        nc.vector.memset(rows2[:], 0.0)
         nc.vector.memset(warm[:], 1.0)
         nc.vector.memset(w2s[:].bitcast(I32), 0)
-        nc.vector.memset(rows2[:], 0.0)
         make_identity(nc, ident_f[:])
         make_identity(nc, ident_b[:])
 
@@ -70,13 +71,13 @@ def tile_mlp_w_kernel(tc, x, in_mean, in_std, out_mean, out_std, W1_words, W1_sc
         with nc.allow_non_contiguous_dma(reason="four neighbouring elements to a partition"):
             nc.scalar.dma_start(out=mean4[:], in_=in_mean.rearrange("(p t) -> p t", t=4))
             nc.scalar.dma_start(out=std4[:], in_=in_std.rearrange("(p t) -> p t", t=4))
-        nc.scalar.dma_start(out=rows1[0:NG, :], in_=b1.rearrange("(g n) -> g n", g=NG))
+            nc.scalar.dma_start(out=b1t[:], in_=b1.rearrange("(g p t) -> p g t", g=NG, t=4))
         nc.scalar.activation(out=warm2[:], in_=warm[:], func=ACT.Abs_reciprocal_sqrt)
 
         w1_dram = W1_words[0].rearrange("p n t -> p (n t)")
 
         def load_w1(i):
-            nc.sync.dma_start(out=w1[:, 1024 * i:1024 * (i + 1)].bitcast(I32),
+            nc.sync.dma_start(out=w1r[:, 1024 * i:1024 * (i + 1)].bitcast(I32),
                               in_=w1_dram[:, 4096 * i:4096 * (i + 1)].bitcast(I32))
 
         def load_w2(i):
@@ -86,7 +87,7 @@ def tile_mlp_w_kernel(tc, x, in_mean, in_std, out_mean, out_std, W1_words, W1_sc
         def load_w1s():
             for q in range(4):
                 nc.sync.dma_start(
-                    out=w1s[32 * q:32 * q + 16, :].bitcast(I32),
+                    out=w1sr[32 * q:32 * q + 16, :].bitcast(I32),
                     in_=W1_scales[0, 4 * q:4 * q + 4, :].rearrange("r (c n) -> c r n", c=4).bitcast(I32))
 
         def load_w2s(b):
@@ -103,169 +104,136 @@ def tile_mlp_w_kernel(tc, x, in_mean, in_std, out_mean, out_std, W1_words, W1_sc
         load_w1s()
         load_rows2()
         load_w1(1)
-        load_w1(2)
-        load_w1(3)
-        nc.sync.dma_start(out=bias[:, 4096:6144], in_=b1[4096:6144].partition_broadcast(P))
         load_w2s(0)
         load_w2(0)
-        load_w1(4)
+        load_w1(2)
         load_w2(1)
-        load_w1(5)
+        load_w1(3)
         load_w2s(1)
         load_w2(2)
-        nc.sync.dma_start(out=bias[:, 6144:8192], in_=b1[6144:8192].partition_broadcast(P))
-        load_w1(6)
+        load_w1(4)
         load_w2(3)
+        load_w1(5)
         load_w2s(2)
-        load_w1(7)
         load_w2(4)
+        load_w1(6)
         load_w2(5)
+        load_w1(7)
         load_w2s(3)
         load_w2(6)
         load_w2(7)
 
+        def permute_scales(j):
+            nc.vector.tensor_copy(out=w1sp[:, 512 * j:512 * (j + 1)].rearrange("p (t m) -> p t m", t=4),
+                                  in_=w1sr[:, 512 * j:512 * (j + 1)].rearrange("p (m t) -> p t m", t=4))
+
+        def permute(g):
+            nc.vector.tensor_copy(
+                out=w1p[:, 512 * g:512 * (g + 1)].bitcast(I32).rearrange("p (t m) -> p t m", t=4),
+                in_=w1r[:, 512 * g:512 * (g + 1)].bitcast(I32).rearrange("p (m t) -> p t m", t=4))
+
         nc.vector.tensor_tensor(out=dvec[:], in0=ident_b[:, 1:2], in1=ident_b[:, 0:1], op=ALU.subtract)
         nc.vector.reciprocal(out=rstd4[:], in_=std4[:])
+        permute_scales(0)
 
-        def spread_bias(i, tag):
-            bp = psum.tile([P, 1024], BF16, name="bp%d" % i, tag=tag)
-            for hh in range(2):
-                g = 2 * i + hh
-                nc.tensor.matmul(out=bp[:, 512 * hh:512 * (hh + 1)], lhsT=ident_b[:, g:g + 1].to_broadcast([P, P]),
-                                 rhs=rows1[:], start=True, stop=True)
-            nc.scalar.copy(out=bias[:, 1024 * i:1024 * (i + 1)], in_=bp[:])
-
-        xT = psum.tile([P, 2 * NT, P], F32, name="xT", tag="tr0")
+        xT = psum.tile([P, 2 * NT, P], F32, name="xT", tag="l1_5")
         for tt in range(NT):
             xw = x_sb[:, tt, :].bitcast(F32)
             for u in range(2):
                 nc.tensor.transpose(out=xT[:, 2 * tt + u, :], in_=xw[:, u:256:2], identity=ident_f[:])
-        spread_bias(0, "acc0")
-        spread_bias(1, "acc1")
-        spread_bias(2, "tr1")
-        spread_bias(3, "acc0")
         for tt in range(NT):
             nc.vector.tensor_tensor(
                 out=xc[:, tt, :].rearrange("p (k u e) -> p k u e", u=2, e=2),
                 in0=xT[:, 2 * tt:2 * tt + 2, :].bitcast(BF16).rearrange("p u (k e) -> p k u e", e=2),
                 in1=mean4[:].rearrange("p (u e) -> p u e", e=2).unsqueeze(1).to_broadcast([P, P, 2, 2]),
                 op=ALU.subtract)
+        for tt in range(NT):
             nc.vector.tensor_tensor(
-                out=xg[:, tt, :].rearrange("p (k t) -> p k t", t=4),
+                out=xg[:, 512 * tt:512 * (tt + 1)].rearrange("p (k t) -> p k t", t=4),
                 in0=xc[:, tt, :].rearrange("p (k t) -> p k t", t=4),
                 in1=rstd4[:].unsqueeze(1).to_broadcast([P, P, 4]),
                 op=ALU.mult)
-            nc.vector.quantize_mx(out=xq[:, P * tt:P * (tt + 1)].bitcast(FP8X4),
-                                  scales=xqs[:, P * tt:P * (tt + 1)], in_=xg[:, tt, :])
+        permute(0)
+        nc.vector.quantize_mx(out=xq[:].bitcast(FP8X4), scales=xqs[:], in_=xg[:])
+        permute(1)
+
+        def spread_row(sel, tag, extra):
+            ps = psum.tile([P, 512], F32, name="ps_" + tag, tag=tag)
+            nc.tensor.matmul(out=ps[:], lhsT=sel.to_broadcast([P, P]), rhs=rows2[:], start=True, stop=(extra is None))
+            if extra is not None:
+                nc.tensor.matmul(out=ps[:], lhsT=ident_b[:], rhs=extra, start=False, stop=True)
+            return ps
+
+        nc.scalar.copy(out=b1f[:], in_=b1t[:].rearrange("p g t -> p (g t)"))
+        ps_b2 = spread_row(ident_b[:, 3:4], "l1_4", None)
+        ps_os = spread_row(ident_b[:, 2:3], "l1_3", None)
+        ps_c = [spread_row(dvec[:, 0:1], "acc%d" % tt, x_sb[:, tt, :]) for tt in range(NT)]
+        nc.scalar.copy(out=b2_sb[:], in_=ps_b2[:])
+        nc.scalar.copy(out=os_sb[:], in_=ps_os[:])
 
         l1_tiles = {}
-        h_tiles = {}
-        tr_tiles = {}
+        hs_tiles = {}
         hg_tiles = {}
         acc = []
 
-        def layer1(g, tt):
-            n = 2 * g + tt
-            t = psum.tile([P, 512], F32, name="l1_%d" % n, tag="l1_%d" % (n % 4))
-            l1_tiles[(g, tt)] = t
+        def layer1(g):
             k = 4 * (g // 4)
             c = 512 * (g % 4)
-            nc.tensor.matmul_mx(out=t[:], lhsT=xq[:, P * tt:P * (tt + 1)].bitcast(FP8X4),
-                                lhsT_scale=xqs[:, P * tt:P * (tt + 1)],
-                                rhs=w1[:, 512 * g:512 * (g + 1)].bitcast(FP8X4),
-                                rhs_scale=w1s[k:P, c:c + 512], start=True, stop=True)
+            for u in range(2):
+                bank = psum.tile([P, 2, B], F32, name="l1_%d_%d" % (g, u), tag="l1_%d" % ((2 * g + u) % 6))
+                l1_tiles[(g, u)] = bank
+                for e in range(2):
+                    t = 2 * u + e
+                    nc.tensor.matmul_mx(out=bank[:, e, :],
+                                        lhsT=w1p[:, 512 * g + P * t:512 * g + P * (t + 1)].bitcast(FP8X4),
+                                        lhsT_scale=w1sp[k:P, c + P * t:c + P * (t + 1)],
+                                        rhs=xq[:].bitcast(FP8X4), rhs_scale=xqs[:], start=True, stop=True)
 
-        def add_bias(g, tt):
-            h = hpool.tile([P, 512], BF16, name="h_%d_%d" % (g, tt), tag="h")
-            h_tiles[(g, tt)] = h
-            nc.vector.tensor_tensor(
-                out=h[:].rearrange("p (t j) -> p t j", t=4),
-                in0=l1_tiles[(g, tt)][:].rearrange("p (j t) -> p t j", t=4),
-                in1=bias[:, 512 * g:512 * (g + 1)].rearrange("p (j t) -> p t j", t=4),
-                op=ALU.add)
+        def evacuate(g):
+            hs = spool.tile([P, 4, B], BF16, name="hs_%d" % g, tag="hs")
+            hs_tiles[g] = hs
+            for t in range(4):
+                nc.scalar.activation(out=hs[:, t, :], in_=l1_tiles[(g, t // 2)][:, t % 2, :], func=ACT.Relu,
+                                     bias=b1f[:, 4 * g + t:4 * g + t + 1])
 
-        def transposes(g):
-            t = psum.tile([P, 4, B], BF16, name="tr_%d" % g, tag="tr%d" % (g % 2))
-            tr_tiles[g] = t
-            for tt in range(NT):
-                for j in range(4):
-                    nc.tensor.transpose(out=t[:, j, P * tt:P * (tt + 1)],
-                                        in_=h_tiles[(g, tt)][:, P * j:P * (j + 1)], identity=ident_b[:])
-
-        def relu(g, engine):
+        def interleave(g):
             hg = gpool.tile([P, 4 * B], BF16, name="hg_%d" % g, tag="hg", align_bytes=64)
             hg_tiles[g] = hg
-            dst = hg[:].rearrange("p (k t) -> p k t", t=4)
-            src = tr_tiles[g][:].rearrange("p t k -> p k t")
-            if engine == "scalar":
-                nc.scalar.activation(out=dst, in_=src, func=ACT.Relu)
-            else:
-                nc.vector.tensor_scalar_max(out=dst, in0=src, scalar1=0.0)
+            nc.vector.tensor_copy(out=hg[:].rearrange("p (c t) -> p c t", t=4),
+                                  in_=hs_tiles[g][:].rearrange("p t c -> p c t"))
 
         def quantise(g):
             nc.vector.quantize_mx(out=hq[:, g, :].bitcast(FP8X4), scales=hqs[:, g, :], in_=hg_tiles[g][:])
 
-        def layer2(g, tiles):
+        def layer2(g):
             k = 4 * (g % 4)
             c = 512 * (g // 4)
-            for tt in tiles:
+            if g == 0:
+                for tt in range(NT):
+                    acc.append(psum.tile([P, 512], F32, name="acc%d" % tt, tag="acc%d" % tt))
+            for tt in range(NT):
                 nc.tensor.matmul_mx(out=acc[tt][:], lhsT=hq[:, g, P * tt:P * (tt + 1)].bitcast(FP8X4),
                                     lhsT_scale=hqs[:, g, P * tt:P * (tt + 1)],
                                     rhs=w2[:, g, :].bitcast(FP8X4), rhs_scale=w2s[k:P, c:c + 512],
                                     start=(g == 0), stop=(g == NG - 1))
 
-        def spread_row(sel, dst, tag):
-            ps = psum.tile([P, 512], F32, name="ps_" + tag, tag=tag)
-            nc.tensor.matmul(out=ps[:], lhsT=sel.to_broadcast([P, P]), rhs=rows2[:], start=True, stop=True)
-            nc.scalar.copy(out=dst[:], in_=ps[:])
-
-        for g in (0, 1):
-            for tt in range(NT):
-                layer1(g, tt)
-        for g in (0, 1):
-            for tt in range(NT):
-                add_bias(g, tt)
-        for g in (2, 3):
-            for tt in range(NT):
-                layer1(g, tt)
-        spread_row(ident_b[:, 3:4], b2_sb, "tr1")
-        spread_row(ident_b[:, 2:3], os_sb, "acc0")
-        ps_d = psum.tile([P, 512], F32, name="ps_d", tag="acc1")
-        nc.tensor.matmul(out=ps_d[:], lhsT=dvec[:, 0:1].to_broadcast([P, P]), rhs=rows2[:], start=True, stop=True)
-        for g in (2, 3):
-            for tt in range(NT):
-                add_bias(g, tt)
-        for tt in range(NT):
-            nc.vector.tensor_tensor(out=c_sb[tt][:], in0=ps_d[:], in1=x_sb[:, tt, :], op=ALU.add)
-
-        NS = NG // 2
-        for s in range(NS):
-            nxt = [(g, tt) for g in (2 * s + 2, 2 * s + 3) for tt in range(NT)] if 1 <= s < NS - 1 else []
-            for g, tt in nxt:
-                layer1(g, tt)
-            for g, tt in nxt:
-                add_bias(g, tt)
-            if s >= 1:
-                quantise(2 * s - 2)
-                quantise(2 * s - 1)
-            transposes(2 * s)
-            transposes(2 * s + 1)
-            relu(2 * s, "scalar")
-            relu(2 * s + 1, "vector" if s == NS - 1 else "scalar")
-            if s == 2:
+        for i in range(NG + LAG):
+            if i < NG:
+                layer1(i)
+                evacuate(i)
+            if i == 0:
                 for tt in range(NT):
-                    acc.append(psum.tile([P, 512], F32, name="acc%d" % tt, tag="acc%d" % tt))
-            if s >= 2:
-                layer2(2 * s - 4, (0, 1))
-                layer2(2 * s - 3, (0, 1))
-        layer2(NG - 4, (0, 1))
-        layer2(NG - 3, (0, 1))
-        quantise(NG - 2)
-        quantise(NG - 1)
-        layer2(NG - 2, (0,))
-        layer2(NG - 1, (0,))
-        layer2(NG - 2, (1,))
-        layer2(NG - 1, (1,))
+                    nc.scalar.copy(out=c_sb[tt][:], in_=ps_c[tt][:])
+            if 1 <= i <= NG:
+                interleave(i - 1)
+            if i + LEAD < NG:
+                permute(i + LEAD)
+            if i + 1 < 4:
+                permute_scales(i + 1)
+            if 1 <= i <= NG:
+                quantise(i - 1)
+            if i >= LAG:
+                layer2(i - LAG)
 
         nm2 = float(norm_max) * float(norm_max)
         res, rr, mp, ot, junk = [], [], [], [], []

@@ -18,8 +18,9 @@ NT = B // P
 NG = D_HID // 512
 EPS = 1e-12
 FLOPS = 2 * B * D_IN * D_HID + 2 * B * D_HID * D_OUT
+UNITS = [[0], [1]] + [[g, g + 1] for g in range(2, NG - 2, 2)] + [[NG - 2], [NG - 1]]
 LEAD = 2
-LAG = 3
+LAG = 2
 
 
 def tile_mlp_w_kernel(tc, x, in_mean, in_std, out_mean, out_std, W1_words, W1_scales, b1,
@@ -127,10 +128,11 @@ def tile_mlp_w_kernel(tc, x, in_mean, in_std, out_mean, out_std, W1_words, W1_sc
             nc.vector.tensor_copy(out=w1sp[:, 512 * j:512 * (j + 1)].rearrange("p (t m) -> p t m", t=4),
                                   in_=w1sr[:, 512 * j:512 * (j + 1)].rearrange("p (m t) -> p t m", t=4))
 
-        def permute(g):
+        def permute(unit):
+            lo, hi = 512 * unit[0], 512 * (unit[-1] + 1)
             nc.vector.tensor_copy(
-                out=w1p[:, 512 * g:512 * (g + 1)].bitcast(I32).rearrange("p (t m) -> p t m", t=4),
-                in_=w1r[:, 512 * g:512 * (g + 1)].bitcast(I32).rearrange("p (m t) -> p t m", t=4))
+                out=w1p[:, lo:hi].bitcast(I32).rearrange("p (g t m) -> p g t m", t=4, m=P),
+                in_=w1r[:, lo:hi].bitcast(I32).rearrange("p (g m t) -> p g t m", t=4, m=P))
 
         nc.vector.tensor_tensor(out=dvec[:], in0=ident_b[:, 1:2], in1=ident_b[:, 0:1], op=ALU.subtract)
         nc.vector.reciprocal(out=rstd4[:], in_=std4[:])
@@ -153,9 +155,9 @@ def tile_mlp_w_kernel(tc, x, in_mean, in_std, out_mean, out_std, W1_words, W1_sc
                 in0=xc[:, tt, :].rearrange("p (k t) -> p k t", t=4),
                 in1=rstd4[:].unsqueeze(1).to_broadcast([P, P, 4]),
                 op=ALU.mult)
-        permute(0)
+        permute(UNITS[0])
         nc.vector.quantize_mx(out=xq[:].bitcast(FP8X4), scales=xqs[:], in_=xg[:])
-        permute(1)
+        permute(UNITS[1])
 
         def spread_row(sel, tag, extra):
             ps = psum.tile([P, 512], F32, name="ps_" + tag, tag=tag)
@@ -189,21 +191,23 @@ def tile_mlp_w_kernel(tc, x, in_mean, in_std, out_mean, out_std, W1_words, W1_sc
                                         lhsT_scale=w1sp[k:P, c + P * t:c + P * (t + 1)],
                                         rhs=xq[:].bitcast(FP8X4), rhs_scale=xqs[:], start=True, stop=True)
 
-        def evacuate(g):
-            hs = spool.tile([P, 4, B], BF16, name="hs_%d" % g, tag="hs")
-            hs_tiles[g] = hs
+        def evacuate(k, g):
+            if g == UNITS[k][0]:
+                hs_tiles[k] = spool.tile([P, len(UNITS[k]), 4, B], BF16, name="hs_%d" % k, tag="hs")
             for t in range(4):
-                nc.scalar.activation(out=hs[:, t, :], in_=l1_tiles[(g, t // 2)][:, t % 2, :], func=ACT.Relu,
-                                     bias=b1f[:, 4 * g + t:4 * g + t + 1])
+                nc.scalar.activation(out=hs_tiles[k][:, g - UNITS[k][0], t, :], in_=l1_tiles[(g, t // 2)][:, t % 2, :],
+                                     func=ACT.Relu, bias=b1f[:, 4 * g + t:4 * g + t + 1])
 
-        def interleave(g):
-            hg = gpool.tile([P, 4 * B], BF16, name="hg_%d" % g, tag="hg", align_bytes=64)
-            hg_tiles[g] = hg
-            nc.vector.tensor_copy(out=hg[:].rearrange("p (c t) -> p c t", t=4),
-                                  in_=hs_tiles[g][:].rearrange("p t c -> p c t"))
+        def interleave(k):
+            hg = gpool.tile([P, len(UNITS[k]) * 4 * B], BF16, name="hg_%d" % k, tag="hg", align_bytes=64)
+            hg_tiles[k] = hg
+            nc.vector.tensor_copy(out=hg[:].rearrange("p (g c t) -> p g c t", t=4, c=B),
+                                  in_=hs_tiles[k][:].rearrange("p g t c -> p g c t"))
 
-        def quantise(g):
-            nc.vector.quantize_mx(out=hq[:, g, :].bitcast(FP8X4), scales=hqs[:, g, :], in_=hg_tiles[g][:])
+        def quantise(k):
+            lo, hi = UNITS[k][0], UNITS[k][-1] + 1
+            nc.vector.quantize_mx(out=hq[:, lo:hi, :].rearrange("p g c -> p (g c)").bitcast(FP8X4),
+                                  scales=hqs[:, lo:hi, :].rearrange("p g c -> p (g c)"), in_=hg_tiles[k][:])
 
         def layer2(g):
             k = 4 * (g % 4)
@@ -217,23 +221,27 @@ def tile_mlp_w_kernel(tc, x, in_mean, in_std, out_mean, out_std, W1_words, W1_sc
                                     rhs=w2[:, g, :].bitcast(FP8X4), rhs_scale=w2s[k:P, c:c + 512],
                                     start=(g == 0), stop=(g == NG - 1))
 
-        for i in range(NG + LAG):
-            if i < NG:
-                layer1(i)
-                evacuate(i)
-            if i == 0:
+        NU = len(UNITS)
+        for k in range(NU + LAG):
+            if k < NU:
+                for g in UNITS[k]:
+                    layer1(g)
+                    evacuate(k, g)
+            if k == 0:
                 for tt in range(NT):
                     nc.scalar.copy(out=c_sb[tt][:], in_=ps_c[tt][:])
-            if 1 <= i <= NG:
-                interleave(i - 1)
-            if i + LEAD < NG:
-                permute(i + LEAD)
-            if i + 1 < 4:
-                permute_scales(i + 1)
-            if 1 <= i <= NG:
-                quantise(i - 1)
-            if i >= LAG:
-                layer2(i - LAG)
+            if 1 <= k <= NU:
+                interleave(k - 1)
+            if k + LEAD < NU:
+                permute(UNITS[k + LEAD])
+            if k == 0:
+                for j in range(1, 4):
+                    permute_scales(j)
+            if 1 <= k <= NU:
+                quantise(k - 1)
+            if k >= LAG:
+                for g in UNITS[k - LAG]:
+                    layer2(g)
 
         nm2 = float(norm_max) * float(norm_max)
         res, rr, mp, ot, junk = [], [], [], [], []

@@ -37,6 +37,8 @@ def tile_mlp_w_kernel(tc, x, in_mean, in_std, out_mean, out_std, W1_words, W1_sc
         mean4 = keep.tile([P, 4], BF16, name="mean4")
         std4 = keep.tile([P, 4], BF16, name="std4")
         rstd4 = keep.tile([P, 4], F32, name="rstd4")
+        meanf = keep.tile([P, 4], F32, name="meanf")
+        nmr4 = keep.tile([P, 4], F32, name="nmr4")
         ident_f = keep.tile([P, P], F32, name="ident_f")
         ident_b = keep.tile([P, P], BF16, name="ident_b")
         dvec = keep.tile([P, 1], BF16, name="dvec")
@@ -49,7 +51,7 @@ def tile_mlp_w_kernel(tc, x, in_mean, in_std, out_mean, out_std, W1_words, W1_sc
         w2s = keep.tile([P, 2048], U8, name="w2s", align_bytes=64)
         b1t = keep.tile([P, NG, 4], BF16, name="b1t")
         b1f = keep.tile([P, NG * 4], F32, name="b1f")
-        xc = keep.tile([P, NT, 512], F32, name="xc")
+        xs = keep.tile([P, 4, B], BF16, name="xs")
         xg = keep.tile([P, NT * 512], BF16, name="xg", align_bytes=64)
         xq = keep.tile([P, B], U32, name="xq", align_bytes=64)
         xqs = keep.tile([P, B], U8, name="xqs", align_bytes=64)
@@ -61,8 +63,8 @@ def tile_mlp_w_kernel(tc, x, in_mean, in_std, out_mean, out_std, W1_words, W1_sc
         os_sb = keep.tile([P, D_OUT], F32, name="os_sb")
         c_sb = [keep.tile([P, D_OUT], F32, name="c_sb%d" % tt) for tt in range(NT)]
 
-        nc.vector.memset(w1sr[:].bitcast(I32), 0)
         nc.vector.memset(rows2[:], 0.0)
+        nc.vector.memset(w1sr[:].bitcast(I32), 0)
         nc.vector.memset(warm[:], 1.0)
         nc.vector.memset(w2s[:].bitcast(I32), 0)
         make_identity(nc, ident_f[:])
@@ -101,9 +103,9 @@ def tile_mlp_w_kernel(tc, x, in_mean, in_std, out_mean, out_std, W1_words, W1_sc
             for r, v in enumerate((in_mean, out_mean, out_std, b2)):
                 nc.sync.dma_start(out=rows2[r:r + 1, :], in_=v.unsqueeze(0))
 
+        load_rows2()
         load_w1(0)
         load_w1s()
-        load_rows2()
         load_w1(1)
         load_w2s(0)
         load_w2(0)
@@ -136,26 +138,25 @@ def tile_mlp_w_kernel(tc, x, in_mean, in_std, out_mean, out_std, W1_words, W1_sc
 
         nc.vector.tensor_tensor(out=dvec[:], in0=ident_b[:, 1:2], in1=ident_b[:, 0:1], op=ALU.subtract)
         nc.vector.reciprocal(out=rstd4[:], in_=std4[:])
-        permute_scales(0)
+        nc.vector.tensor_copy(out=meanf[:], in_=mean4[:])
+        nc.vector.scalar_tensor_tensor(out=nmr4[:], in0=meanf[:], scalar=-1.0, in1=rstd4[:], op0=ALU.mult, op1=ALU.mult)
 
-        xT = psum.tile([P, 2 * NT, P], F32, name="xT", tag="l1_5")
-        for tt in range(NT):
-            xw = x_sb[:, tt, :].bitcast(F32)
-            for u in range(2):
-                nc.tensor.transpose(out=xT[:, 2 * tt + u, :], in_=xw[:, u:256:2], identity=ident_f[:])
-        for tt in range(NT):
-            nc.vector.tensor_tensor(
-                out=xc[:, tt, :].rearrange("p (k u e) -> p k u e", u=2, e=2),
-                in0=xT[:, 2 * tt:2 * tt + 2, :].bitcast(BF16).rearrange("p u (k e) -> p k u e", e=2),
-                in1=mean4[:].rearrange("p (u e) -> p u e", e=2).unsqueeze(1).to_broadcast([P, P, 2, 2]),
-                op=ALU.subtract)
-        for tt in range(NT):
-            nc.vector.tensor_tensor(
-                out=xg[:, 512 * tt:512 * (tt + 1)].rearrange("p (k t) -> p k t", t=4),
-                in0=xc[:, tt, :].rearrange("p (k t) -> p k t", t=4),
-                in1=rstd4[:].unsqueeze(1).to_broadcast([P, P, 4]),
-                op=ALU.mult)
+        xT = [psum.tile([P, NT, P], F32, name="xT%d" % u, tag="l1_%d" % (5 - 3 * u)) for u in range(2)]
+        for u in range(2):
+            for tt in range(NT):
+                nc.tensor.transpose(out=xT[u][:, tt, :], in_=x_sb[:, tt, :].bitcast(F32)[:, u:256:2], identity=ident_f[:])
+        for t in range(4):
+            src = xT[t // 2][:].bitcast(BF16).rearrange("p tt (k e) -> p e tt k", e=2)[:, t % 2]
+            dst = xs[:, t, :].rearrange("p (tt k) -> p tt k", tt=NT)
+            if t < 2:
+                nc.vector.tensor_scalar(out=dst, in0=src, scalar1=meanf[:, t:t + 1],
+                                        scalar2=rstd4[:, t:t + 1], op0=ALU.subtract, op1=ALU.mult)
+            else:
+                nc.scalar.activation(out=dst, in_=src, func=ACT.Identity,
+                                     scale=rstd4[:, t:t + 1], bias=nmr4[:, t:t + 1])
         permute(UNITS[0])
+        nc.vector.tensor_copy(out=xg[:].rearrange("p (c t) -> p c t", t=4), in_=xs[:].rearrange("p t c -> p c t"))
+        permute_scales(0)
         nc.vector.quantize_mx(out=xq[:].bitcast(FP8X4), scales=xqs[:], in_=xg[:])
         permute(UNITS[1])
 

@@ -194,16 +194,17 @@ def tile_mlp_w_kernel(tc, x, in_mean, in_std, out_mean, out_std, W1_words, W1_sc
 
         def evacuate(k, g):
             if g == UNITS[k][0]:
-                hs_tiles[k] = spool.tile([P, len(UNITS[k]), 4, B], BF16, name="hs_%d" % k, tag="hs")
+                hs_tiles[k] = spool.tile([P, 4, len(UNITS[k]) * B], BF16, name="hs_%d" % k, tag="hs")
+            lo = B * (g - UNITS[k][0])
             for t in range(4):
-                nc.scalar.activation(out=hs_tiles[k][:, g - UNITS[k][0], t, :], in_=l1_tiles[(g, t // 2)][:, t % 2, :],
+                nc.scalar.activation(out=hs_tiles[k][:, t, lo:lo + B], in_=l1_tiles[(g, t // 2)][:, t % 2, :],
                                      func=ACT.Relu, bias=b1f[:, 4 * g + t:4 * g + t + 1])
 
         def interleave(k):
             hg = gpool.tile([P, len(UNITS[k]) * 4 * B], BF16, name="hg_%d" % k, tag="hg", align_bytes=64)
             hg_tiles[k] = hg
-            nc.vector.tensor_copy(out=hg[:].rearrange("p (g c t) -> p g c t", t=4, c=B),
-                                  in_=hs_tiles[k][:].rearrange("p g t c -> p g c t"))
+            nc.vector.tensor_copy(out=hg[:].rearrange("p (c i t) -> p c t i", i=4, t=4),
+                                  in_=hs_tiles[k][:].rearrange("p t (c i) -> p c t i", i=4))
 
         def quantise(k):
             lo, hi = UNITS[k][0], UNITS[k][-1] + 1

@@ -20,7 +20,7 @@ EPS = 1e-12
 FLOPS = 2 * B * D_IN * D_HID + 2 * B * D_HID * D_OUT
 UNITS = [[0], [1]] + [[g, g + 1] for g in range(2, NG - 2, 2)] + [[NG - 2], [NG - 1]]
 LEAD = 2
-LAG = 2
+LAG = 3
 
 
 def tile_mlp_w_kernel(tc, x, in_mean, in_std, out_mean, out_std, W1_words, W1_scales, b1,
@@ -107,21 +107,21 @@ def tile_mlp_w_kernel(tc, x, in_mean, in_std, out_mean, out_std, W1_words, W1_sc
         load_w1(0)
         load_w1s()
         load_w1(1)
+        load_w1(2)
+        load_w1(3)
         load_w2s(0)
         load_w2(0)
-        load_w1(2)
+        load_w1(4)
         load_w2(1)
-        load_w1(3)
+        load_w1(5)
         load_w2s(1)
         load_w2(2)
-        load_w1(4)
+        load_w1(6)
         load_w2(3)
-        load_w1(5)
+        load_w1(7)
         load_w2s(2)
         load_w2(4)
-        load_w1(6)
         load_w2(5)
-        load_w1(7)
         load_w2s(3)
         load_w2(6)
         load_w2(7)
@@ -239,8 +239,8 @@ def tile_mlp_w_kernel(tc, x, in_mean, in_std, out_mean, out_std, W1_words, W1_sc
             if k == 0:
                 for j in range(1, 4):
                     permute_scales(j)
-            if 1 <= k <= NU:
-                quantise(k - 1)
+            if 2 <= k <= NU + 1:
+                quantise(k - 2)
             if k >= LAG:
                 for g in UNITS[k - LAG]:
                     layer2(g)

@@ -133,8 +133,8 @@ def tile_mlp_w_kernel(tc, x, in_mean, in_std, out_mean, out_std, W1_words, W1_sc
         def permute(unit):
             lo, hi = 512 * unit[0], 512 * (unit[-1] + 1)
             nc.vector.tensor_copy(
-                out=w1p[:, lo:hi].bitcast(I32).rearrange("p (g t m) -> p g t m", t=4, m=P),
-                in_=w1r[:, lo:hi].bitcast(I32).rearrange("p (g m t) -> p g t m", t=4, m=P))
+                out=w1p[:, lo:hi].bitcast(I32).rearrange("p (t c i) -> p c t i", t=4, i=4),
+                in_=w1r[:, lo:hi].bitcast(I32).rearrange("p (c i t) -> p c t i", t=4, i=4))
 
         nc.vector.tensor_tensor(out=dvec[:], in0=ident_b[:, 1:2], in1=ident_b[:, 0:1], op=ALU.subtract)
         nc.vector.reciprocal(out=rstd4[:], in_=std4[:])
@@ -179,7 +179,7 @@ def tile_mlp_w_kernel(tc, x, in_mean, in_std, out_mean, out_std, W1_words, W1_sc
         hg_tiles = {}
         acc = []
 
-        def layer1(g):
+        def layer1(unit, g):
             k = 4 * (g // 4)
             c = 512 * (g % 4)
             for u in range(2):
@@ -187,8 +187,9 @@ def tile_mlp_w_kernel(tc, x, in_mean, in_std, out_mean, out_std, W1_words, W1_sc
                 l1_tiles[(g, u)] = bank
                 for e in range(2):
                     t = 2 * u + e
+                    col = 512 * unit[0] + P * (len(unit) * t + g - unit[0])
                     nc.tensor.matmul_mx(out=bank[:, e, :],
-                                        lhsT=w1p[:, 512 * g + P * t:512 * g + P * (t + 1)].bitcast(FP8X4),
+                                        lhsT=w1p[:, col:col + P].bitcast(FP8X4),
                                         lhsT_scale=w1sp[k:P, c + P * t:c + P * (t + 1)],
                                         rhs=xq[:].bitcast(FP8X4), rhs_scale=xqs[:], start=True, stop=True)
 
@@ -227,7 +228,7 @@ def tile_mlp_w_kernel(tc, x, in_mean, in_std, out_mean, out_std, W1_words, W1_sc
         for k in range(NU + LAG):
             if k < NU:
                 for g in UNITS[k]:
-                    layer1(g)
+                    layer1(UNITS[k], g)
                     evacuate(k, g)
             if k == 0:
                 for tt in range(NT):

@@ -59,8 +59,8 @@ def tile_mlp_w_kernel(tc, x, in_mean, in_std, out_mean, out_std, W1_words, W1_sc
         hqs = keep.tile([P, NG, B], U8, name="hqs", align_bytes=64)
         warm = keep.tile([P, 1], F32, name="warm")
         warm2 = keep.tile([P, 1], F32, name="warm2")
-        b2_sb = keep.tile([P, D_OUT], F32, name="b2_sb")
-        os_sb = keep.tile([P, D_OUT], F32, name="os_sb")
+        b2_bc = keep.tile([P, D_OUT], BF16, name="b2_bc")
+        os_bc = keep.tile([P, D_OUT], BF16, name="os_bc")
         c_sb = [keep.tile([P, D_OUT], F32, name="c_sb%d" % tt) for tt in range(NT)]
 
         nc.vector.memset(rows2[:], 0.0)
@@ -100,8 +100,12 @@ def tile_mlp_w_kernel(tc, x, in_mean, in_std, out_mean, out_std, W1_words, W1_sc
                     in_=W2_scales[4 * b:4 * b + 4, 4 * q:4 * q + 4, :].bitcast(I32))
 
         def load_rows2():
-            for r, v in enumerate((in_mean, out_mean, out_std, b2)):
+            for r, v in enumerate((in_mean, out_mean)):
                 nc.sync.dma_start(out=rows2[r:r + 1, :], in_=v.unsqueeze(0))
+
+        def load_spread():
+            nc.sync.dma_start(out=b2_bc[:], in_=b2.partition_broadcast(P))
+            nc.sync.dma_start(out=os_bc[:], in_=out_std.partition_broadcast(P))
 
         load_rows2()
         load_w1(0)
@@ -119,6 +123,7 @@ def tile_mlp_w_kernel(tc, x, in_mean, in_std, out_mean, out_std, W1_words, W1_sc
         load_w1(6)
         load_w2(3)
         load_w1(7)
+        load_spread()
         load_w2s(2)
         load_w2(4)
         load_w2(5)
@@ -126,9 +131,9 @@ def tile_mlp_w_kernel(tc, x, in_mean, in_std, out_mean, out_std, W1_words, W1_sc
         load_w2(6)
         load_w2(7)
 
-        def permute_scales(j):
-            nc.vector.tensor_copy(out=w1sp[:, 512 * j:512 * (j + 1)].rearrange("p (t m) -> p t m", t=4),
-                                  in_=w1sr[:, 512 * j:512 * (j + 1)].rearrange("p (m t) -> p t m", t=4))
+        def permute_scales(j0, j1):
+            nc.vector.tensor_copy(out=w1sp[:].rearrange("p (t x i) -> p x t i", t=4, i=16)[:, 8 * j0:8 * j1],
+                                  in_=w1sr[:, 512 * j0:512 * j1].rearrange("p (x i t) -> p x t i", i=16, t=4))
 
         def permute(unit):
             lo, hi = 512 * unit[0], 512 * (unit[-1] + 1)
@@ -156,7 +161,7 @@ def tile_mlp_w_kernel(tc, x, in_mean, in_std, out_mean, out_std, W1_words, W1_sc
                                      scale=rstd4[:, t:t + 1], bias=nmr4[:, t:t + 1])
         permute(UNITS[0])
         nc.vector.tensor_copy(out=xg[:].rearrange("p (c t) -> p c t", t=4), in_=xs[:].rearrange("p t c -> p c t"))
-        permute_scales(0)
+        permute_scales(0, 1)
         nc.vector.quantize_mx(out=xq[:].bitcast(FP8X4), scales=xqs[:], in_=xg[:])
         permute(UNITS[1])
 
@@ -168,11 +173,9 @@ def tile_mlp_w_kernel(tc, x, in_mean, in_std, out_mean, out_std, W1_words, W1_sc
             return ps
 
         nc.scalar.copy(out=b1f[:], in_=b1t[:].rearrange("p g t -> p (g t)"))
-        ps_b2 = spread_row(ident_b[:, 3:4], "l1_4", None)
-        ps_os = spread_row(ident_b[:, 2:3], "l1_3", None)
         ps_c = [spread_row(dvec[:, 0:1], "acc%d" % tt, x_sb[:, tt, :]) for tt in range(NT)]
-        nc.scalar.copy(out=b2_sb[:], in_=ps_b2[:])
-        nc.scalar.copy(out=os_sb[:], in_=ps_os[:])
+        for tt in range(NT):
+            nc.scalar.copy(out=c_sb[tt][:], in_=ps_c[tt][:])
 
         l1_tiles = {}
         hs_tiles = {}
@@ -181,7 +184,7 @@ def tile_mlp_w_kernel(tc, x, in_mean, in_std, out_mean, out_std, W1_words, W1_sc
 
         def layer1(unit, g):
             k = 4 * (g // 4)
-            c = 512 * (g % 4)
+            c = P * (g % 4)
             for u in range(2):
                 bank = psum.tile([P, 2, B], F32, name="l1_%d_%d" % (g, u), tag="l1_%d" % ((2 * g + u) % 6))
                 l1_tiles[(g, u)] = bank
@@ -190,7 +193,7 @@ def tile_mlp_w_kernel(tc, x, in_mean, in_std, out_mean, out_std, W1_words, W1_sc
                     col = 512 * unit[0] + P * (len(unit) * t + g - unit[0])
                     nc.tensor.matmul_mx(out=bank[:, e, :],
                                         lhsT=w1p[:, col:col + P].bitcast(FP8X4),
-                                        lhsT_scale=w1sp[k:P, c + P * t:c + P * (t + 1)],
+                                        lhsT_scale=w1sp[k:P, 512 * t + c:512 * t + c + P],
                                         rhs=xq[:].bitcast(FP8X4), rhs_scale=xqs[:], start=True, stop=True)
 
         def evacuate(k, g):
@@ -230,16 +233,12 @@ def tile_mlp_w_kernel(tc, x, in_mean, in_std, out_mean, out_std, W1_words, W1_sc
                 for g in UNITS[k]:
                     layer1(UNITS[k], g)
                     evacuate(k, g)
-            if k == 0:
-                for tt in range(NT):
-                    nc.scalar.copy(out=c_sb[tt][:], in_=ps_c[tt][:])
             if 1 <= k <= NU:
                 interleave(k - 1)
+            if k == 0:
+                permute_scales(1, 4)
             if k + LEAD < NU:
                 permute(UNITS[k + LEAD])
-            if k == 0:
-                for j in range(1, 4):
-                    permute_scales(j)
             if 2 <= k <= NU + 1:
                 quantise(k - 2)
             if k >= LAG:
@@ -259,14 +258,14 @@ def tile_mlp_w_kernel(tc, x, in_mean, in_std, out_mean, out_std, W1_words, W1_sc
                 lst.append(keep.tile([P, 1], F32, name="%s_%d" % (nm, tt)))
 
         def end_add(tt):
-            nc.vector.tensor_tensor(out=res[tt][:], in0=acc[tt][:], in1=b2_sb[:], op=ALU.add)
+            nc.vector.tensor_tensor(out=res[tt][:], in0=acc[tt][:], in1=b2_bc[:], op=ALU.add)
 
         def end_norm1(tt):
             nc.scalar.activation(out=junk[tt][:], in_=res[tt][:], func=ACT.Square, accum_out=n2[tt][:])
             nc.scalar.activation(out=f0[tt][:], in_=n2[tt][:], func=ACT.Abs_reciprocal_sqrt, scale=1.0 / nm2)
 
         def end_gain(tt):
-            nc.vector.tensor_tensor(out=rr[tt][:], in0=res[tt][:], in1=os_sb[:], op=ALU.mult)
+            nc.vector.tensor_tensor(out=rr[tt][:], in0=res[tt][:], in1=os_bc[:], op=ALU.mult)
 
         def end_map(tt):
             nc.vector.tensor_scalar_min(out=fac[tt][:], in0=f0[tt][:], scalar1=1.0)

@@ -50,7 +50,6 @@ def tile_mlp_w_kernel(tc, x, in_mean, in_std, out_mean, out_std, W1_words, W1_sc
         w1sp = keep.tile([P, 2048], U8, name="w1sp", align_bytes=64)
         w2s = keep.tile([P, 2048], U8, name="w2s", align_bytes=64)
         b1t = keep.tile([P, NG, 4], BF16, name="b1t")
-        b1f = keep.tile([P, NG * 4], F32, name="b1f")
         xs = keep.tile([P, 4, B], BF16, name="xs")
         xg = keep.tile([P, NT * 512], BF16, name="xg", align_bytes=64)
         xq = keep.tile([P, B], U32, name="xq", align_bytes=64)
@@ -74,7 +73,8 @@ def tile_mlp_w_kernel(tc, x, in_mean, in_std, out_mean, out_std, W1_words, W1_sc
         with nc.allow_non_contiguous_dma(reason="four neighbouring elements to a partition"):
             nc.scalar.dma_start(out=mean4[:], in_=in_mean.rearrange("(p t) -> p t", t=4))
             nc.scalar.dma_start(out=std4[:], in_=in_std.rearrange("(p t) -> p t", t=4))
-            nc.scalar.dma_start(out=b1t[:], in_=b1.rearrange("(g p t) -> p g t", g=NG, t=4))
+            nc.scalar.dma_start(out=b1t[:, 0:4, :], in_=b1[0:2048].rearrange("(g p t) -> p g t", g=4, t=4))
+            nc.scalar.dma_start(out=b1t[:, 4:NG, :], in_=b1[2048:D_HID].rearrange("(g p t) -> p g t", g=NG - 4, t=4))
         nc.scalar.activation(out=warm2[:], in_=warm[:], func=ACT.Abs_reciprocal_sqrt)
 
         w1_dram = W1_words[0].rearrange("p n t -> p (n t)")
@@ -172,7 +172,6 @@ def tile_mlp_w_kernel(tc, x, in_mean, in_std, out_mean, out_std, W1_words, W1_sc
                 nc.tensor.matmul(out=ps[:], lhsT=ident_b[:], rhs=extra, start=False, stop=True)
             return ps
 
-        nc.scalar.copy(out=b1f[:], in_=b1t[:].rearrange("p g t -> p (g t)"))
         ps_c = [spread_row(dvec[:, 0:1], "acc%d" % tt, x_sb[:, tt, :]) for tt in range(NT)]
         for tt in range(NT):
             nc.scalar.copy(out=c_sb[tt][:], in_=ps_c[tt][:])
@@ -202,7 +201,7 @@ def tile_mlp_w_kernel(tc, x, in_mean, in_std, out_mean, out_std, W1_words, W1_sc
             lo = B * (g - UNITS[k][0])
             for t in range(4):
                 nc.scalar.activation(out=hs_tiles[k][:, t, lo:lo + B], in_=l1_tiles[(g, t // 2)][:, t % 2, :],
-                                     func=ACT.Relu, bias=b1f[:, 4 * g + t:4 * g + t + 1])
+                                     func=ACT.Relu, bias=b1t[:, g, t:t + 1])
 
         def interleave(k):
             hg = gpool.tile([P, len(UNITS[k]) * 4 * B], BF16, name="hg_%d" % k, tag="hg", align_bytes=64)

@@ -19,8 +19,9 @@ NG = D_HID // 512
 EPS = 1e-12
 FLOPS = 2 * B * D_IN * D_HID + 2 * B * D_HID * D_OUT
 UNITS = [[0], [1]] + [[g, g + 1] for g in range(2, NG - 2, 2)] + [[NG - 2], [NG - 1]]
+PARTS = [(u, 0, B) for u in UNITS[:-1]] + [(UNITS[-1], P * tt, P * (tt + 1)) for tt in range(NT)]
 LEAD = 2
-LAG = 3
+LAG = 2
 
 
 def tile_mlp_w_kernel(tc, x, in_mean, in_std, out_mean, out_std, W1_words, W1_scales, b1,
@@ -50,20 +51,19 @@ def tile_mlp_w_kernel(tc, x, in_mean, in_std, out_mean, out_std, W1_words, W1_sc
         w1sp = keep.tile([P, 2048], U8, name="w1sp", align_bytes=64)
         w2s = keep.tile([P, 2048], U8, name="w2s", align_bytes=64)
         b1t = keep.tile([P, NG, 4], BF16, name="b1t")
-        xs = keep.tile([P, 4, B], BF16, name="xs")
+        xs = [keep.tile([P, 4, P], BF16, name="xs%d" % tt) for tt in range(NT)]
         xg = keep.tile([P, NT * 512], BF16, name="xg", align_bytes=64)
         xq = keep.tile([P, B], U32, name="xq", align_bytes=64)
         xqs = keep.tile([P, B], U8, name="xqs", align_bytes=64)
-        hq = keep.tile([P, NG, B], U32, name="hq", align_bytes=64)
-        hqs = keep.tile([P, NG, B], U8, name="hqs", align_bytes=64)
+        hq = keep.tile([P, NG * B], U32, name="hq", align_bytes=64)
+        hqs = keep.tile([P, NG * B], U8, name="hqs", align_bytes=64)
         warm = keep.tile([P, 1], F32, name="warm")
         warm2 = keep.tile([P, 1], F32, name="warm2")
         b2_bc = keep.tile([P, D_OUT], BF16, name="b2_bc")
         os_bc = keep.tile([P, D_OUT], BF16, name="os_bc")
-        c_sb = [keep.tile([P, D_OUT], F32, name="c_sb%d" % tt) for tt in range(NT)]
 
+        nc.gpsimd.memset(w1sr[:].bitcast(I32), 0)
         nc.vector.memset(rows2[:], 0.0)
-        nc.vector.memset(w1sr[:].bitcast(I32), 0)
         nc.vector.memset(warm[:], 1.0)
         nc.vector.memset(w2s[:].bitcast(I32), 0)
         make_identity(nc, ident_f[:])
@@ -71,27 +71,32 @@ def tile_mlp_w_kernel(tc, x, in_mean, in_std, out_mean, out_std, W1_words, W1_sc
 
         nc.scalar.dma_start(out=x_sb[:], in_=x.rearrange("(tt p) k -> p tt k", p=P))
         with nc.allow_non_contiguous_dma(reason="four neighbouring elements to a partition"):
-            nc.scalar.dma_start(out=mean4[:], in_=in_mean.rearrange("(p t) -> p t", t=4))
-            nc.scalar.dma_start(out=std4[:], in_=in_std.rearrange("(p t) -> p t", t=4))
-            nc.scalar.dma_start(out=b1t[:, 0:4, :], in_=b1[0:2048].rearrange("(g p t) -> p g t", g=4, t=4))
-            nc.scalar.dma_start(out=b1t[:, 4:NG, :], in_=b1[2048:D_HID].rearrange("(g p t) -> p g t", g=NG - 4, t=4))
+            nc.sync.dma_start(out=std4[:], in_=in_std.rearrange("(p t) -> p t", t=4))
+            nc.sync.dma_start(out=mean4[:], in_=in_mean.rearrange("(p t) -> p t", t=4))
         nc.scalar.activation(out=warm2[:], in_=warm[:], func=ACT.Abs_reciprocal_sqrt)
 
         w1_dram = W1_words[0].rearrange("p n t -> p (n t)")
 
-        def load_w1(i):
-            nc.sync.dma_start(out=w1r[:, 1024 * i:1024 * (i + 1)].bitcast(I32),
-                              in_=w1_dram[:, 4096 * i:4096 * (i + 1)].bitcast(I32))
+        def load_w1(i, n=2):
+            g = int(2 * i)
+            nc.sync.dma_start(out=w1r[:, 512 * g:512 * (g + n)].bitcast(I32),
+                              in_=w1_dram[:, 2048 * g:2048 * (g + n)].bitcast(I32))
+
+        def load_b1(g0, g1):
+            with nc.allow_non_contiguous_dma(reason="four neighbouring elements to a partition"):
+                nc.scalar.dma_start(out=b1t[:, g0:g1, :],
+                                    in_=b1[512 * g0:512 * g1].rearrange("(g p t) -> p g t", g=g1 - g0, t=4))
 
         def load_w2(i):
             nc.sync.dma_start(out=w2[:, 2 * i:2 * i + 2, :].bitcast(I32),
                               in_=W2_words[2 * i:2 * i + 2].rearrange("g p n t -> p g (n t)").bitcast(I32))
 
-        def load_w1s():
+        def load_w1s(j0, j1, g0):
+            n = 512 * (j1 - j0)
             for q in range(4):
                 nc.sync.dma_start(
-                    out=w1sr[32 * q:32 * q + 16, :].bitcast(I32),
-                    in_=W1_scales[0, 4 * q:4 * q + 4, :].rearrange("r (c n) -> c r n", c=4).bitcast(I32))
+                    out=w1sr[32 * q:32 * q + 16, 512 * j0:512 * j1].bitcast(I32),
+                    in_=W1_scales[0, 4 * q:4 * q + 4, 512 * g0:512 * g0 + 4 * n].rearrange("r (c n) -> c r n", c=4).bitcast(I32))
 
         def load_w2s(b):
             for q in range(4):
@@ -99,18 +104,19 @@ def tile_mlp_w_kernel(tc, x, in_mean, in_std, out_mean, out_std, W1_words, W1_sc
                     out=w2s[32 * q:32 * q + 16, 512 * b:512 * (b + 1)].bitcast(I32),
                     in_=W2_scales[4 * b:4 * b + 4, 4 * q:4 * q + 4, :].bitcast(I32))
 
-        def load_rows2():
+        def load_spread():
             for r, v in enumerate((in_mean, out_mean)):
                 nc.sync.dma_start(out=rows2[r:r + 1, :], in_=v.unsqueeze(0))
-
-        def load_spread():
             nc.sync.dma_start(out=b2_bc[:], in_=b2.partition_broadcast(P))
             nc.sync.dma_start(out=os_bc[:], in_=out_std.partition_broadcast(P))
 
-        load_rows2()
-        load_w1(0)
-        load_w1s()
+        load_w1(0, 1)
+        load_w1s(0, 1, 0)
+        load_b1(0, 4)
+        load_w1(0.5, 1)
         load_w1(1)
+        load_b1(4, NG)
+        load_w1s(1, 4, 4)
         load_w1(2)
         load_w1(3)
         load_w2s(0)
@@ -146,35 +152,34 @@ def tile_mlp_w_kernel(tc, x, in_mean, in_std, out_mean, out_std, W1_words, W1_sc
         nc.vector.tensor_copy(out=meanf[:], in_=mean4[:])
         nc.vector.scalar_tensor_tensor(out=nmr4[:], in0=meanf[:], scalar=-1.0, in1=rstd4[:], op0=ALU.mult, op1=ALU.mult)
 
-        xT = [psum.tile([P, NT, P], F32, name="xT%d" % u, tag="l1_%d" % (5 - 3 * u)) for u in range(2)]
-        for u in range(2):
-            for tt in range(NT):
-                nc.tensor.transpose(out=xT[u][:, tt, :], in_=x_sb[:, tt, :].bitcast(F32)[:, u:256:2], identity=ident_f[:])
-        for t in range(4):
-            src = xT[t // 2][:].bitcast(BF16).rearrange("p tt (k e) -> p e tt k", e=2)[:, t % 2]
-            dst = xs[:, t, :].rearrange("p (tt k) -> p tt k", tt=NT)
-            if t < 2:
-                nc.vector.tensor_scalar(out=dst, in0=src, scalar1=meanf[:, t:t + 1],
-                                        scalar2=rstd4[:, t:t + 1], op0=ALU.subtract, op1=ALU.mult)
-            else:
-                nc.scalar.activation(out=dst, in_=src, func=ACT.Identity,
-                                     scale=rstd4[:, t:t + 1], bias=nmr4[:, t:t + 1])
+        xT = [[psum.tile([P, P], F32, name="xT%d_%d" % (tt, u), tag="l1_%d" % (2 + 2 * tt + u)) for u in range(2)]
+              for tt in range(NT)]
+        for tt in range(NT):
+            for u in range(2):
+                nc.tensor.transpose(out=xT[tt][u][:], in_=x_sb[:, tt, :].bitcast(F32)[:, u:256:2], identity=ident_f[:])
+        for tt in range(NT):
+            for t in range(4):
+                src = xT[tt][t // 2][:].bitcast(BF16).rearrange("p (k e) -> p e k", e=2)[:, t % 2]
+                dst = xs[tt][:, t, :]
+                if t < 2:
+                    nc.vector.tensor_scalar(out=dst, in0=src, scalar1=meanf[:, t:t + 1],
+                                            scalar2=rstd4[:, t:t + 1], op0=ALU.subtract, op1=ALU.mult)
+                else:
+                    nc.scalar.activation(out=dst, in_=src, func=ACT.Identity,
+                                         scale=rstd4[:, t:t + 1], bias=nmr4[:, t:t + 1])
         permute(UNITS[0])
-        nc.vector.tensor_copy(out=xg[:].rearrange("p (c t) -> p c t", t=4), in_=xs[:].rearrange("p t c -> p c t"))
+        for tt in range(NT):
+            nc.vector.tensor_copy(out=xg[:, 512 * tt:512 * (tt + 1)].rearrange("p (c i t) -> p c t i", i=4, t=4),
+                                  in_=xs[tt][:].rearrange("p t (c i) -> p c t i", i=4))
         permute_scales(0, 1)
         nc.vector.quantize_mx(out=xq[:].bitcast(FP8X4), scales=xqs[:], in_=xg[:])
         permute(UNITS[1])
 
-        def spread_row(sel, tag, extra):
-            ps = psum.tile([P, 512], F32, name="ps_" + tag, tag=tag)
-            nc.tensor.matmul(out=ps[:], lhsT=sel.to_broadcast([P, P]), rhs=rows2[:], start=True, stop=(extra is None))
-            if extra is not None:
-                nc.tensor.matmul(out=ps[:], lhsT=ident_b[:], rhs=extra, start=False, stop=True)
+        def spread_row(tt):
+            ps = psum.tile([P, 512], F32, name="ps_c%d" % tt, tag="l1_%d" % (2 * NG % 6 + tt))
+            nc.tensor.matmul(out=ps[:], lhsT=dvec[:, 0:1].to_broadcast([P, P]), rhs=rows2[:], start=True, stop=False)
+            nc.tensor.matmul(out=ps[:], lhsT=ident_b[:], rhs=x_sb[:, tt, :], start=False, stop=True)
             return ps
-
-        ps_c = [spread_row(dvec[:, 0:1], "acc%d" % tt, x_sb[:, tt, :]) for tt in range(NT)]
-        for tt in range(NT):
-            nc.scalar.copy(out=c_sb[tt][:], in_=ps_c[tt][:])
 
         l1_tiles = {}
         hs_tiles = {}
@@ -182,8 +187,8 @@ def tile_mlp_w_kernel(tc, x, in_mean, in_std, out_mean, out_std, W1_words, W1_sc
         acc = []
 
         def layer1(unit, g):
-            k = 4 * (g // 4)
-            c = P * (g % 4)
+            k = 4 * (g if g < 4 else (g - 4) // 3)
+            c = P * (0 if g < 4 else 1 + (g - 4) % 3)
             for u in range(2):
                 bank = psum.tile([P, 2, B], F32, name="l1_%d_%d" % (g, u), tag="l1_%d" % ((2 * g + u) % 6))
                 l1_tiles[(g, u)] = bank
@@ -195,54 +200,64 @@ def tile_mlp_w_kernel(tc, x, in_mean, in_std, out_mean, out_std, W1_words, W1_sc
                                         lhsT_scale=w1sp[k:P, 512 * t + c:512 * t + c + P],
                                         rhs=xq[:].bitcast(FP8X4), rhs_scale=xqs[:], start=True, stop=True)
 
-        def evacuate(k, g):
-            if g == UNITS[k][0]:
-                hs_tiles[k] = spool.tile([P, 4, len(UNITS[k]) * B], BF16, name="hs_%d" % k, tag="hs")
-            lo = B * (g - UNITS[k][0])
-            for t in range(4):
-                nc.scalar.activation(out=hs_tiles[k][:, t, lo:lo + B], in_=l1_tiles[(g, t // 2)][:, t % 2, :],
-                                     func=ACT.Relu, bias=b1t[:, g, t:t + 1])
+        def part_columns(k):
+            units, lo, hi = PARTS[k]
+            return B * units[0] + len(units) * lo, hi - lo
+
+        def evacuate(k):
+            groups, lo, hi = PARTS[k]
+            n = hi - lo
+            hs_tiles[k] = spool.tile([P, 4, len(groups) * n], BF16, name="hs_%d" % k, tag="hs")
+            for j, g in enumerate(groups):
+                if lo == 0:
+                    layer1(groups, g)
+                for t in range(4):
+                    nc.scalar.activation(out=hs_tiles[k][:, t, n * j:n * (j + 1)], in_=l1_tiles[(g, t // 2)][:, t % 2, lo:hi],
+                                         func=ACT.Relu, bias=b1t[:, g, t:t + 1])
 
         def interleave(k):
-            hg = gpool.tile([P, len(UNITS[k]) * 4 * B], BF16, name="hg_%d" % k, tag="hg", align_bytes=64)
+            groups, lo, hi = PARTS[k]
+            hg = gpool.tile([P, len(groups) * 4 * (hi - lo)], BF16, name="hg_%d" % k, tag="hg", align_bytes=64)
             hg_tiles[k] = hg
             nc.vector.tensor_copy(out=hg[:].rearrange("p (c i t) -> p c t i", i=4, t=4),
                                   in_=hs_tiles[k][:].rearrange("p t (c i) -> p c t i", i=4))
 
         def quantise(k):
-            lo, hi = UNITS[k][0], UNITS[k][-1] + 1
-            nc.vector.quantize_mx(out=hq[:, lo:hi, :].rearrange("p g c -> p (g c)").bitcast(FP8X4),
-                                  scales=hqs[:, lo:hi, :].rearrange("p g c -> p (g c)"), in_=hg_tiles[k][:])
+            c, n = part_columns(k)
+            c1 = c + len(PARTS[k][0]) * n
+            nc.vector.quantize_mx(out=hq[:, c:c1].bitcast(FP8X4), scales=hqs[:, c:c1], in_=hg_tiles[k][:])
 
-        def layer2(g):
-            k = 4 * (g % 4)
-            c = 512 * (g // 4)
-            if g == 0:
-                for tt in range(NT):
-                    acc.append(psum.tile([P, 512], F32, name="acc%d" % tt, tag="acc%d" % tt))
-            for tt in range(NT):
-                nc.tensor.matmul_mx(out=acc[tt][:], lhsT=hq[:, g, P * tt:P * (tt + 1)].bitcast(FP8X4),
-                                    lhsT_scale=hqs[:, g, P * tt:P * (tt + 1)],
-                                    rhs=w2[:, g, :].bitcast(FP8X4), rhs_scale=w2s[k:P, c:c + 512],
-                                    start=(g == 0), stop=(g == NG - 1))
+        def layer2(k):
+            groups, lo, hi = PARTS[k]
+            c0, n = part_columns(k)
+            for j, g in enumerate(groups):
+                row = 4 * (g % 4)
+                b = 512 * (g // 4)
+                if g == 0:
+                    for tt in range(NT):
+                        acc.append(psum.tile([P, 512], F32, name="acc%d" % tt, tag="acc%d" % tt))
+                for tt in range(lo // P, hi // P):
+                    c = c0 + n * j + P * tt - lo
+                    nc.tensor.matmul_mx(out=acc[tt][:], lhsT=hq[:, c:c + P].bitcast(FP8X4), lhsT_scale=hqs[:, c:c + P],
+                                        rhs=w2[:, g, :].bitcast(FP8X4), rhs_scale=w2s[row:P, b:b + 512],
+                                        start=(g == 0), stop=(g == NG - 1))
 
-        NU = len(UNITS)
-        for k in range(NU + LAG):
-            if k < NU:
-                for g in UNITS[k]:
-                    layer1(UNITS[k], g)
-                    evacuate(k, g)
-            if 1 <= k <= NU:
+        NK = len(PARTS)
+        for k in range(NK + LAG):
+            if k < NK:
+                evacuate(k)
+            if 1 <= k <= NK:
                 interleave(k - 1)
-            if k == 0:
-                permute_scales(1, 4)
-            if k + LEAD < NU:
+            if k + LEAD < len(UNITS):
                 permute(UNITS[k + LEAD])
-            if 2 <= k <= NU + 1:
-                quantise(k - 2)
+            if k == 1:
+                permute_scales(1, 4)
+            if 1 <= k <= NK:
+                quantise(k - 1)
+            if k == NK - 1:
+                ps_c = [spread_row(tt) for tt in range(NT)]
             if k >= LAG:
-                for g in UNITS[k - LAG]:
-                    layer2(g)
+                layer2(k - LAG)
 
         nm2 = float(norm_max) * float(norm_max)
         res, rr, mp, ot, junk = [], [], [], [], []
@@ -268,7 +283,7 @@ def tile_mlp_w_kernel(tc, x, in_mean, in_std, out_mean, out_std, W1_words, W1_sc
 
         def end_map(tt):
             nc.vector.tensor_scalar_min(out=fac[tt][:], in0=f0[tt][:], scalar1=1.0)
-            nc.vector.scalar_tensor_tensor(out=mp[tt][:], in0=rr[tt][:], scalar=fac[tt][:, 0:1], in1=c_sb[tt][:],
+            nc.vector.scalar_tensor_tensor(out=mp[tt][:], in0=rr[tt][:], scalar=fac[tt][:, 0:1], in1=ps_c[tt][:],
                                            op0=ALU.mult, op1=ALU.add)
 
         def end_norm2(tt):

@@ -44,6 +44,7 @@ def tile_mlp_w_kernel(tc, x, in_mean, in_std, out_mean, out_std, W1_words, W1_sc
         ident_b = keep.tile([P, P], BF16, name="ident_b")
         dvec = keep.tile([P, 1], BF16, name="dvec")
         rows2 = keep.tile([P, 512], BF16, name="rows2")
+        vrows = keep.tile([P, 512], BF16, name="vrows")
         w1r = keep.tile([P, D_HID], U32, name="w1r", align_bytes=64)
         w1p = keep.tile([P, D_HID], U32, name="w1p", align_bytes=64)
         w2 = keep.tile([P, NG, D_OUT], U32, name="w2", align_bytes=64)
@@ -62,17 +63,19 @@ def tile_mlp_w_kernel(tc, x, in_mean, in_std, out_mean, out_std, W1_words, W1_sc
         b2_bc = keep.tile([P, D_OUT], BF16, name="b2_bc")
         os_bc = keep.tile([P, D_OUT], BF16, name="os_bc")
 
-        nc.gpsimd.memset(w1sr[:].bitcast(I32), 0)
-        nc.vector.memset(rows2[:], 0.0)
+        nc.gpsimd.memset(vrows[:], 0.0)
+        nc.vector.memset(w1sr[:].bitcast(I32), 0)
         nc.vector.memset(warm[:], 1.0)
+        nc.vector.memset(rows2[:], 0.0)
         nc.vector.memset(w2s[:].bitcast(I32), 0)
         make_identity(nc, ident_f[:])
         make_identity(nc, ident_b[:])
 
         nc.scalar.dma_start(out=x_sb[:], in_=x.rearrange("(tt p) k -> p tt k", p=P))
         with nc.allow_non_contiguous_dma(reason="four neighbouring elements to a partition"):
-            nc.sync.dma_start(out=std4[:], in_=in_std.rearrange("(p t) -> p t", t=4))
-            nc.sync.dma_start(out=mean4[:], in_=in_mean.rearrange("(p t) -> p t", t=4))
+            nc.scalar.dma_start(out=std4[:], in_=in_std.rearrange("(p t) -> p t", t=4))
+            nc.scalar.dma_start(out=mean4[:], in_=in_mean.rearrange("(p t) -> p t", t=4))
+        nc.scalar.dma_start(out=vrows[0:NG, :], in_=b1.rearrange("(g k) -> g k", g=NG))
         nc.scalar.activation(out=warm2[:], in_=warm[:], func=ACT.Abs_reciprocal_sqrt)
 
         w1_dram = W1_words[0].rearrange("p n t -> p (n t)")
@@ -81,11 +84,6 @@ def tile_mlp_w_kernel(tc, x, in_mean, in_std, out_mean, out_std, W1_words, W1_sc
             g = int(2 * i)
             nc.sync.dma_start(out=w1r[:, 512 * g:512 * (g + n)].bitcast(I32),
                               in_=w1_dram[:, 2048 * g:2048 * (g + n)].bitcast(I32))
-
-        def load_b1(g0, g1):
-            with nc.allow_non_contiguous_dma(reason="four neighbouring elements to a partition"):
-                nc.scalar.dma_start(out=b1t[:, g0:g1, :],
-                                    in_=b1[512 * g0:512 * g1].rearrange("(g p t) -> p g t", g=g1 - g0, t=4))
 
         def load_w2(i):
             nc.sync.dma_start(out=w2[:, 2 * i:2 * i + 2, :].bitcast(I32),
@@ -112,10 +110,8 @@ def tile_mlp_w_kernel(tc, x, in_mean, in_std, out_mean, out_std, W1_words, W1_sc
 
         load_w1(0, 1)
         load_w1s(0, 1, 0)
-        load_b1(0, 4)
         load_w1(0.5, 1)
         load_w1(1)
-        load_b1(4, NG)
         load_w1s(1, 4, 4)
         load_w1(2)
         load_w1(3)
@@ -167,6 +163,12 @@ def tile_mlp_w_kernel(tc, x, in_mean, in_std, out_mean, out_std, W1_words, W1_sc
                 else:
                     nc.scalar.activation(out=dst, in_=src, func=ACT.Identity,
                                          scale=rstd4[:, t:t + 1], bias=nmr4[:, t:t + 1])
+        bT = psum.tile([P, 2, P], F32, name="bT", tag="l1_0")
+        for u in range(2):
+            nc.tensor.transpose(out=bT[:, u, :], in_=vrows[:].bitcast(F32)[:, u:256:2], identity=ident_f[:])
+        b4 = bT[:].rearrange("p u r -> p (u r)").bitcast(BF16).rearrange("p (u r e) -> p r u e", u=2, e=2)
+        nc.scalar.copy(out=b1t[:].rearrange("p g (u e) -> p g u e", u=2), in_=b4[:, 0:NG])
+
         permute(UNITS[0])
         for tt in range(NT):
             nc.vector.tensor_copy(out=xg[:, 512 * tt:512 * (tt + 1)].rearrange("p (c i t) -> p c t i", i=4, t=4),

@@ -62,28 +62,30 @@ def tile_mlp_w_kernel(tc, x, in_mean, in_std, out_mean, out_std, W1_words, W1_sc
         warm2 = keep.tile([P, 1], F32, name="warm2")
         b2_bc = keep.tile([P, D_OUT], BF16, name="b2_bc")
         os_bc = keep.tile([P, D_OUT], BF16, name="os_bc")
+        c_sb = [keep.tile([P, D_OUT], F32, name="c_sb%d" % tt) for tt in range(NT)]
 
-        nc.gpsimd.memset(vrows[:], 0.0)
+        nc.vector.memset(rows2[:], 0.0)
+        nc.vector.memset(vrows[:], 0.0)
         nc.vector.memset(w1sr[:].bitcast(I32), 0)
         nc.vector.memset(warm[:], 1.0)
-        nc.vector.memset(rows2[:], 0.0)
         nc.vector.memset(w2s[:].bitcast(I32), 0)
         make_identity(nc, ident_f[:])
-        make_identity(nc, ident_b[:])
+        nc.gpsimd.dma_start(out=rows2[1:2, :], in_=out_mean.unsqueeze(0))
+        nc.vector.tensor_copy(out=ident_b[:], in_=ident_f[:])
 
-        nc.scalar.dma_start(out=x_sb[:], in_=x.rearrange("(tt p) k -> p tt k", p=P))
+        nc.sync.dma_start(out=x_sb[:], in_=x.rearrange("(tt p) k -> p tt k", p=P))
         with nc.allow_non_contiguous_dma(reason="four neighbouring elements to a partition"):
             nc.scalar.dma_start(out=std4[:], in_=in_std.rearrange("(p t) -> p t", t=4))
             nc.scalar.dma_start(out=mean4[:], in_=in_mean.rearrange("(p t) -> p t", t=4))
+        nc.scalar.dma_start(out=rows2[0:1, :], in_=in_mean.unsqueeze(0))
         nc.scalar.dma_start(out=vrows[0:NG, :], in_=b1.rearrange("(g k) -> g k", g=NG))
         nc.scalar.activation(out=warm2[:], in_=warm[:], func=ACT.Abs_reciprocal_sqrt)
 
         w1_dram = W1_words[0].rearrange("p n t -> p (n t)")
 
-        def load_w1(i, n=2):
-            g = int(2 * i)
-            nc.sync.dma_start(out=w1r[:, 512 * g:512 * (g + n)].bitcast(I32),
-                              in_=w1_dram[:, 2048 * g:2048 * (g + n)].bitcast(I32))
+        def load_w1(i):
+            nc.sync.dma_start(out=w1r[:, 1024 * i:1024 * (i + 1)].bitcast(I32),
+                              in_=w1_dram[:, 4096 * i:4096 * (i + 1)].bitcast(I32))
 
         def load_w2(i):
             nc.sync.dma_start(out=w2[:, 2 * i:2 * i + 2, :].bitcast(I32),
@@ -103,17 +105,14 @@ def tile_mlp_w_kernel(tc, x, in_mean, in_std, out_mean, out_std, W1_words, W1_sc
                     in_=W2_scales[4 * b:4 * b + 4, 4 * q:4 * q + 4, :].bitcast(I32))
 
         def load_spread():
-            for r, v in enumerate((in_mean, out_mean)):
-                nc.sync.dma_start(out=rows2[r:r + 1, :], in_=v.unsqueeze(0))
             nc.sync.dma_start(out=b2_bc[:], in_=b2.partition_broadcast(P))
             nc.sync.dma_start(out=os_bc[:], in_=out_std.partition_broadcast(P))
 
-        load_w1(0, 1)
+        load_w1(0)
         load_w1s(0, 1, 0)
-        load_w1(0.5, 1)
         load_w1(1)
-        load_w1s(1, 4, 4)
         load_w1(2)
+        load_w1s(1, 4, 4)
         load_w1(3)
         load_w2s(0)
         load_w2(0)
@@ -177,11 +176,13 @@ def tile_mlp_w_kernel(tc, x, in_mean, in_std, out_mean, out_std, W1_words, W1_sc
         nc.vector.quantize_mx(out=xq[:].bitcast(FP8X4), scales=xqs[:], in_=xg[:])
         permute(UNITS[1])
 
-        def spread_row(tt):
-            ps = psum.tile([P, 512], F32, name="ps_c%d" % tt, tag="l1_%d" % (2 * NG % 6 + tt))
-            nc.tensor.matmul(out=ps[:], lhsT=dvec[:, 0:1].to_broadcast([P, P]), rhs=rows2[:], start=True, stop=False)
-            nc.tensor.matmul(out=ps[:], lhsT=ident_b[:], rhs=x_sb[:, tt, :], start=False, stop=True)
-            return ps
+        ps_c = [psum.tile([P, 512], F32, name="ps_c%d" % tt, tag="acc%d" % tt) for tt in range(NT)]
+        for tt in range(NT):
+            nc.tensor.matmul(out=ps_c[tt][:], lhsT=ident_b[:], rhs=x_sb[:, tt, :], start=True, stop=False)
+        for tt in range(NT):
+            nc.tensor.matmul(out=ps_c[tt][:], lhsT=dvec[:, 0:1].to_broadcast([P, P]), rhs=rows2[:], start=False, stop=True)
+        for tt in range(NT):
+            nc.scalar.copy(out=c_sb[tt][:], in_=ps_c[tt][:])
 
         l1_tiles = {}
         hs_tiles = {}
@@ -256,8 +257,6 @@ def tile_mlp_w_kernel(tc, x, in_mean, in_std, out_mean, out_std, W1_words, W1_sc
                 permute_scales(1, 4)
             if 1 <= k <= NK:
                 quantise(k - 1)
-            if k == NK - 1:
-                ps_c = [spread_row(tt) for tt in range(NT)]
             if k >= LAG:
                 layer2(k - LAG)
 
@@ -285,7 +284,7 @@ def tile_mlp_w_kernel(tc, x, in_mean, in_std, out_mean, out_std, W1_words, W1_sc
 
         def end_map(tt):
             nc.vector.tensor_scalar_min(out=fac[tt][:], in0=f0[tt][:], scalar1=1.0)
-            nc.vector.scalar_tensor_tensor(out=mp[tt][:], in0=rr[tt][:], scalar=fac[tt][:, 0:1], in1=ps_c[tt][:],
+            nc.vector.scalar_tensor_tensor(out=mp[tt][:], in0=rr[tt][:], scalar=fac[tt][:, 0:1], in1=c_sb[tt][:],
                                            op0=ALU.mult, op1=ALU.add)
 
         def end_norm2(tt):

@@ -65,35 +65,37 @@ def tile_mlp_w_kernel(tc, x, in_mean, in_std, out_mean, out_std, W1_words, W1_sc
         c_sb = [keep.tile([P, D_OUT], F32, name="c_sb%d" % tt) for tt in range(NT)]
 
         nc.vector.memset(rows2[:], 0.0)
+        nc.vector.memset(w1sr[:, 0:512].bitcast(I32), 0)
         nc.vector.memset(vrows[:], 0.0)
-        nc.vector.memset(w1sr[:].bitcast(I32), 0)
         nc.vector.memset(warm[:], 1.0)
+        nc.vector.memset(w1sr[:, 512:2048].bitcast(I32), 0)
         nc.vector.memset(w2s[:].bitcast(I32), 0)
         make_identity(nc, ident_f[:])
-        nc.gpsimd.dma_start(out=rows2[1:2, :], in_=out_mean.unsqueeze(0))
         nc.vector.tensor_copy(out=ident_b[:], in_=ident_f[:])
 
-        nc.sync.dma_start(out=x_sb[:], in_=x.rearrange("(tt p) k -> p tt k", p=P))
+        idle = psum.tile([P, 512], F32, name="idle", tag="acc0")
+        for i in range(3):
+            nc.tensor.matmul(out=idle[:], lhsT=vrows[:, 0:P], rhs=vrows[:], start=True, stop=True)
+
         with nc.allow_non_contiguous_dma(reason="four neighbouring elements to a partition"):
             nc.scalar.dma_start(out=std4[:], in_=in_std.rearrange("(p t) -> p t", t=4))
             nc.scalar.dma_start(out=mean4[:], in_=in_mean.rearrange("(p t) -> p t", t=4))
-        nc.scalar.dma_start(out=rows2[0:1, :], in_=in_mean.unsqueeze(0))
-        nc.scalar.dma_start(out=vrows[0:NG, :], in_=b1.rearrange("(g k) -> g k", g=NG))
+        nc.sync.dma_start(out=x_sb[:], in_=x.rearrange("(tt p) k -> p tt k", p=P))
         nc.scalar.activation(out=warm2[:], in_=warm[:], func=ACT.Abs_reciprocal_sqrt)
 
         w1_dram = W1_words[0].rearrange("p n t -> p (n t)")
 
-        def load_w1(i):
-            nc.sync.dma_start(out=w1r[:, 1024 * i:1024 * (i + 1)].bitcast(I32),
-                              in_=w1_dram[:, 4096 * i:4096 * (i + 1)].bitcast(I32))
+        def load_w1(g0, g1):
+            nc.sync.dma_start(out=w1r[:, 512 * g0:512 * g1].bitcast(I32),
+                              in_=w1_dram[:, 2048 * g0:2048 * g1].bitcast(I32))
 
         def load_w2(i):
             nc.sync.dma_start(out=w2[:, 2 * i:2 * i + 2, :].bitcast(I32),
                               in_=W2_words[2 * i:2 * i + 2].rearrange("g p n t -> p g (n t)").bitcast(I32))
 
-        def load_w1s(j0, j1, g0):
+        def load_w1s(j0, j1, g0, quadrants):
             n = 512 * (j1 - j0)
-            for q in range(4):
+            for q in quadrants:
                 nc.sync.dma_start(
                     out=w1sr[32 * q:32 * q + 16, 512 * j0:512 * j1].bitcast(I32),
                     in_=W1_scales[0, 4 * q:4 * q + 4, 512 * g0:512 * g0 + 4 * n].rearrange("r (c n) -> c r n", c=4).bitcast(I32))
@@ -108,22 +110,26 @@ def tile_mlp_w_kernel(tc, x, in_mean, in_std, out_mean, out_std, W1_words, W1_sc
             nc.sync.dma_start(out=b2_bc[:], in_=b2.partition_broadcast(P))
             nc.sync.dma_start(out=os_bc[:], in_=out_std.partition_broadcast(P))
 
-        load_w1(0)
-        load_w1s(0, 1, 0)
-        load_w1(1)
-        load_w1(2)
-        load_w1s(1, 4, 4)
-        load_w1(3)
+        load_w1(0, 1)
+        for r, v in enumerate((in_mean, out_mean)):
+            nc.sync.dma_start(out=rows2[r:r + 1, :], in_=v.unsqueeze(0))
+        load_w1s(0, 1, 0, range(4))
+        nc.sync.dma_start(out=vrows[0:NG, :], in_=b1.rearrange("(g k) -> g k", g=NG))
+        load_w1(1, 2)
+        load_w1(2, 4)
+        load_w1(4, 6)
+        load_w1s(1, 4, 4, range(4))
+        load_w1(6, 8)
         load_w2s(0)
         load_w2(0)
-        load_w1(4)
+        load_w1(8, 10)
         load_w2(1)
-        load_w1(5)
+        load_w1(10, 12)
         load_w2s(1)
         load_w2(2)
-        load_w1(6)
+        load_w1(12, 14)
         load_w2(3)
-        load_w1(7)
+        load_w1(14, 16)
         load_spread()
         load_w2s(2)
         load_w2(4)
@@ -152,6 +158,7 @@ def tile_mlp_w_kernel(tc, x, in_mean, in_std, out_mean, out_std, W1_words, W1_sc
         for tt in range(NT):
             for u in range(2):
                 nc.tensor.transpose(out=xT[tt][u][:], in_=x_sb[:, tt, :].bitcast(F32)[:, u:256:2], identity=ident_f[:])
+        permute(UNITS[0])
         for tt in range(NT):
             for t in range(4):
                 src = xT[tt][t // 2][:].bitcast(BF16).rearrange("p (k e) -> p e k", e=2)[:, t % 2]
@@ -162,16 +169,9 @@ def tile_mlp_w_kernel(tc, x, in_mean, in_std, out_mean, out_std, W1_words, W1_sc
                 else:
                     nc.scalar.activation(out=dst, in_=src, func=ACT.Identity,
                                          scale=rstd4[:, t:t + 1], bias=nmr4[:, t:t + 1])
-        bT = psum.tile([P, 2, P], F32, name="bT", tag="l1_0")
-        for u in range(2):
-            nc.tensor.transpose(out=bT[:, u, :], in_=vrows[:].bitcast(F32)[:, u:256:2], identity=ident_f[:])
-        b4 = bT[:].rearrange("p u r -> p (u r)").bitcast(BF16).rearrange("p (u r e) -> p r u e", u=2, e=2)
-        nc.scalar.copy(out=b1t[:].rearrange("p g (u e) -> p g u e", u=2), in_=b4[:, 0:NG])
-
-        permute(UNITS[0])
-        for tt in range(NT):
-            nc.vector.tensor_copy(out=xg[:, 512 * tt:512 * (tt + 1)].rearrange("p (c i t) -> p c t i", i=4, t=4),
-                                  in_=xs[tt][:].rearrange("p t (c i) -> p c t i", i=4))
+        for tt, copy in enumerate((nc.vector.tensor_copy, nc.scalar.copy)):
+            copy(out=xg[:, 512 * tt:512 * (tt + 1)].rearrange("p (c i t) -> p c t i", i=4, t=4),
+                 in_=xs[tt][:].rearrange("p t (c i) -> p c t i", i=4))
         permute_scales(0, 1)
         nc.vector.quantize_mx(out=xq[:].bitcast(FP8X4), scales=xqs[:], in_=xg[:])
         permute(UNITS[1])
@@ -181,8 +181,13 @@ def tile_mlp_w_kernel(tc, x, in_mean, in_std, out_mean, out_std, W1_words, W1_sc
             nc.tensor.matmul(out=ps_c[tt][:], lhsT=ident_b[:], rhs=x_sb[:, tt, :], start=True, stop=False)
         for tt in range(NT):
             nc.tensor.matmul(out=ps_c[tt][:], lhsT=dvec[:, 0:1].to_broadcast([P, P]), rhs=rows2[:], start=False, stop=True)
+        bT = psum.tile([P, 2, P], F32, name="bT", tag="l1_0")
+        for u in range(2):
+            nc.tensor.transpose(out=bT[:, u, :], in_=vrows[:].bitcast(F32)[:, u:256:2], identity=ident_f[:])
+        b4 = bT[:].rearrange("p u r -> p (u r)").bitcast(BF16).rearrange("p (u r e) -> p r u e", u=2, e=2)
         for tt in range(NT):
             nc.scalar.copy(out=c_sb[tt][:], in_=ps_c[tt][:])
+        nc.scalar.copy(out=b1t[:].rearrange("p g (u e) -> p g u e", u=2), in_=b4[:, 0:NG])
 
         l1_tiles = {}
         hs_tiles = {}
@@ -251,11 +256,14 @@ def tile_mlp_w_kernel(tc, x, in_mean, in_std, out_mean, out_std, W1_words, W1_sc
                 evacuate(k)
             if 1 <= k <= NK:
                 interleave(k - 1)
+            if k == 1:
+                permute_scales(3, 4)
+                quantise(0)
             if k + LEAD < len(UNITS):
                 permute(UNITS[k + LEAD])
-            if k == 1:
-                permute_scales(1, 4)
-            if 1 <= k <= NK:
+            if k == 0:
+                permute_scales(1, 3)
+            if 2 <= k <= NK:
                 quantise(k - 1)
             if k >= LAG:
                 layer2(k - LAG)

@@ -64,9 +64,9 @@ def tile_mlp_w_kernel(tc, x, in_mean, in_std, out_mean, out_std, W1_words, W1_sc
         os_bc = keep.tile([P, D_OUT], BF16, name="os_bc")
         c_sb = [keep.tile([P, D_OUT], F32, name="c_sb%d" % tt) for tt in range(NT)]
 
-        nc.vector.memset(rows2[:], 0.0)
+        nc.gpsimd.memset(vrows[:].bitcast(F32), 0.0)
+        nc.vector.memset(rows2[:].bitcast(I32), 0)
         nc.vector.memset(w1sr[:, 0:512].bitcast(I32), 0)
-        nc.vector.memset(vrows[:], 0.0)
         nc.vector.memset(warm[:], 1.0)
         nc.vector.memset(w1sr[:, 512:2048].bitcast(I32), 0)
         nc.vector.memset(w2s[:].bitcast(I32), 0)
@@ -74,7 +74,7 @@ def tile_mlp_w_kernel(tc, x, in_mean, in_std, out_mean, out_std, W1_words, W1_sc
         nc.vector.tensor_copy(out=ident_b[:], in_=ident_f[:])
 
         idle = psum.tile([P, 512], F32, name="idle", tag="acc0")
-        for i in range(3):
+        for i in range(4):
             nc.tensor.matmul(out=idle[:], lhsT=vrows[:, 0:P], rhs=vrows[:], start=True, stop=True)
 
         with nc.allow_non_contiguous_dma(reason="four neighbouring elements to a partition"):

@@ -117,8 +117,8 @@ def tile_mlp_w_kernel(tc, x, in_mean, in_std, out_mean, out_std, W1_words, W1_sc
         nc.sync.dma_start(out=vrows[0:NG, :], in_=b1.rearrange("(g k) -> g k", g=NG))
         load_w1(1, 2)
         load_w1(2, 4)
-        load_w1(4, 6)
         load_w1s(1, 4, 4, range(4))
+        load_w1(4, 6)
         load_w1(6, 8)
         load_w2s(0)
         load_w2(0)
@@ -169,9 +169,9 @@ def tile_mlp_w_kernel(tc, x, in_mean, in_std, out_mean, out_std, W1_words, W1_sc
                 else:
                     nc.scalar.activation(out=dst, in_=src, func=ACT.Identity,
                                          scale=rstd4[:, t:t + 1], bias=nmr4[:, t:t + 1])
-        for tt, copy in enumerate((nc.vector.tensor_copy, nc.scalar.copy)):
-            copy(out=xg[:, 512 * tt:512 * (tt + 1)].rearrange("p (c i t) -> p c t i", i=4, t=4),
-                 in_=xs[tt][:].rearrange("p t (c i) -> p c t i", i=4))
+        for tt in range(NT):
+            nc.vector.tensor_copy(out=xg[:, 512 * tt:512 * (tt + 1)].rearrange("p (c i t) -> p c t i", i=4, t=4),
+                                  in_=xs[tt][:].rearrange("p t (c i) -> p c t i", i=4))
         permute_scales(0, 1)
         nc.vector.quantize_mx(out=xq[:].bitcast(FP8X4), scales=xqs[:], in_=xg[:])
         permute(UNITS[1])
@@ -251,20 +251,23 @@ def tile_mlp_w_kernel(tc, x, in_mean, in_std, out_mean, out_std, W1_words, W1_sc
                                         start=(g == 0), stop=(g == NG - 1))
 
         NK = len(PARTS)
+        LAST = NK - 1 - NT
         for k in range(NK + LAG):
             if k < NK:
                 evacuate(k)
             if 1 <= k <= NK:
                 interleave(k - 1)
             if k == 1:
-                permute_scales(3, 4)
+                permute_scales(1, 2)
                 quantise(0)
+            if k == 2:
+                permute_scales(2, 4)
             if k + LEAD < len(UNITS):
                 permute(UNITS[k + LEAD])
-            if k == 0:
-                permute_scales(1, 3)
-            if 2 <= k <= NK:
+            if 1 < k <= LAST:
                 quantise(k - 1)
+            if LAST <= k - 2 < NK:
+                quantise(k - 2)
             if k >= LAG:
                 layer2(k - LAG)
 
@@ -280,6 +283,8 @@ def tile_mlp_w_kernel(tc, x, in_mean, in_std, out_mean, out_std, W1_words, W1_sc
             for lst, nm in ((n2, "n2"), (f0, "f0"), (fac, "fac"), (m2, "m2"), (r0, "r0"), (rinv, "rinv")):
                 lst.append(keep.tile([P, 1], F32, name="%s_%d" % (nm, tt)))
 
+        m2b = keep.tile([P, 1], F32, name="m2b")
+
         def end_add(tt):
             nc.vector.tensor_tensor(out=res[tt][:], in0=acc[tt][:], in1=b2_bc[:], op=ALU.add)
 
@@ -290,20 +295,37 @@ def tile_mlp_w_kernel(tc, x, in_mean, in_std, out_mean, out_std, W1_words, W1_sc
         def end_gain(tt):
             nc.vector.tensor_tensor(out=rr[tt][:], in0=res[tt][:], in1=os_bc[:], op=ALU.mult)
 
-        def end_map(tt):
+        def end_clamp(tt):
             nc.vector.tensor_scalar_min(out=fac[tt][:], in0=f0[tt][:], scalar1=1.0)
+
+        def end_map(tt):
             nc.vector.scalar_tensor_tensor(out=mp[tt][:], in0=rr[tt][:], scalar=fac[tt][:, 0:1], in1=c_sb[tt][:],
                                            op0=ALU.mult, op1=ALU.add)
 
         def end_norm2(tt):
-            nc.scalar.activation(out=junk[tt][:], in_=mp[tt][:], func=ACT.Square, accum_out=m2[tt][:])
-            nc.scalar.activation(out=r0[tt][:], in_=m2[tt][:], func=ACT.Abs_reciprocal_sqrt)
+            if tt == NT - 1:
+                half = D_OUT // 2
+                right = mp[tt][:, half:D_OUT]
+                nc.vector.scalar_tensor_tensor(out=rr[tt][:, half:D_OUT], in0=right, scalar=1.0, in1=right,
+                                               op0=ALU.mult, op1=ALU.mult, accum_out=m2b[:])
+                nc.scalar.activation(out=junk[tt][:, 0:half], in_=mp[tt][:, 0:half], func=ACT.Square, accum_out=m2[tt][:])
+                nc.scalar.activation(out=r0[tt][:], in_=m2[tt][:], func=ACT.Abs_reciprocal_sqrt, bias=m2b[:, 0:1])
+            else:
+                nc.scalar.activation(out=junk[tt][:], in_=mp[tt][:], func=ACT.Square, accum_out=m2[tt][:])
+                nc.scalar.activation(out=r0[tt][:], in_=m2[tt][:], func=ACT.Abs_reciprocal_sqrt)
 
         def end_out(tt):
             nc.vector.tensor_scalar_min(out=rinv[tt][:], in0=r0[tt][:], scalar1=1.0 / EPS)
             nc.vector.tensor_scalar_mul(out=ot[tt][:], in0=mp[tt][:], scalar1=rinv[tt][:, 0:1])
             nc.sync.dma_start(out=out[P * tt:P * (tt + 1), :], in_=ot[tt][:])
 
-        for stage in (end_add, end_norm1, end_gain, end_map, end_norm2, end_out):
+        for tt in range(NT):
+            end_add(tt)
+        for tt in range(NT):
+            end_norm1(tt)
+        for tt in range(NT):
+            end_gain(tt)
+            end_clamp(tt)
+        for stage in (end_map, end_norm2, end_out):
             for tt in range(NT):
                 stage(tt)

@@ -60,8 +60,8 @@ def tile_mlp_w_kernel(tc, x, in_mean, in_std, out_mean, out_std, W1_words, W1_sc
         hqs = keep.tile([P, NG * B], U8, name="hqs", align_bytes=64)
         warm = keep.tile([P, 1], F32, name="warm")
         warm2 = keep.tile([P, 1], F32, name="warm2")
-        b2_bc = keep.tile([P, D_OUT], BF16, name="b2_bc")
-        os_bc = keep.tile([P, D_OUT], BF16, name="os_bc")
+        end_rows = keep.tile([P, D_OUT], BF16, name="end_rows")
+        b2_bc = keep.tile([P, D_OUT], F32, name="b2_bc")
         c_sb = [keep.tile([P, D_OUT], F32, name="c_sb%d" % tt) for tt in range(NT)]
 
         nc.gpsimd.memset(vrows[:].bitcast(F32), 0.0)
@@ -70,6 +70,7 @@ def tile_mlp_w_kernel(tc, x, in_mean, in_std, out_mean, out_std, W1_words, W1_sc
         nc.vector.memset(warm[:], 1.0)
         nc.vector.memset(w1sr[:, 512:2048].bitcast(I32), 0)
         nc.vector.memset(w2s[:].bitcast(I32), 0)
+        nc.vector.memset(end_rows[:].bitcast(I32), 0)
         make_identity(nc, ident_f[:])
         nc.vector.tensor_copy(out=ident_b[:], in_=ident_f[:])
 
@@ -106,9 +107,9 @@ def tile_mlp_w_kernel(tc, x, in_mean, in_std, out_mean, out_std, W1_words, W1_sc
                     out=w2s[32 * q:32 * q + 16, 512 * b:512 * (b + 1)].bitcast(I32),
                     in_=W2_scales[4 * b:4 * b + 4, 4 * q:4 * q + 4, :].bitcast(I32))
 
-        def load_spread():
-            nc.sync.dma_start(out=b2_bc[:], in_=b2.partition_broadcast(P))
-            nc.sync.dma_start(out=os_bc[:], in_=out_std.partition_broadcast(P))
+        def load_end_rows():
+            for r, v in enumerate((b2, out_std)):
+                nc.sync.dma_start(out=end_rows[r:r + 1, :], in_=v.unsqueeze(0))
 
         load_w1(0, 1)
         for r, v in enumerate((in_mean, out_mean)):
@@ -130,7 +131,7 @@ def tile_mlp_w_kernel(tc, x, in_mean, in_std, out_mean, out_std, W1_words, W1_sc
         load_w1(12, 14)
         load_w2(3)
         load_w1(14, 16)
-        load_spread()
+        load_end_rows()
         load_w2s(2)
         load_w2(4)
         load_w2(5)
@@ -255,6 +256,13 @@ def tile_mlp_w_kernel(tc, x, in_mean, in_std, out_mean, out_std, W1_words, W1_sc
         for k in range(NK + LAG):
             if k < NK:
                 evacuate(k)
+            if k == NK - 2:
+                spread = [psum.tile([P, D_OUT], F32, name="spread%d" % r, tag="l1_%d" % (2 + r)) for r in range(2)]
+                for r in range(2):
+                    nc.tensor.matmul(out=spread[r][:], lhsT=ident_b[:, r:r + 1].to_broadcast([P, P]), rhs=end_rows[:],
+                                     start=True, stop=True)
+            if k == NK - 1:
+                nc.scalar.copy(out=b2_bc[:], in_=spread[0][:])
             if 1 <= k <= NK:
                 interleave(k - 1)
             if k == 1:
@@ -293,7 +301,7 @@ def tile_mlp_w_kernel(tc, x, in_mean, in_std, out_mean, out_std, W1_words, W1_sc
             nc.scalar.activation(out=f0[tt][:], in_=n2[tt][:], func=ACT.Abs_reciprocal_sqrt, scale=1.0 / nm2)
 
         def end_gain(tt):
-            nc.vector.tensor_tensor(out=rr[tt][:], in0=res[tt][:], in1=os_bc[:], op=ALU.mult)
+            nc.vector.tensor_tensor(out=rr[tt][:], in0=res[tt][:], in1=spread[1][:], op=ALU.mult)
 
         def end_clamp(tt):
             nc.vector.tensor_scalar_min(out=fac[tt][:], in0=f0[tt][:], scalar1=1.0)

@@ -65,24 +65,24 @@ def tile_mlp_w_kernel(tc, x, in_mean, in_std, out_mean, out_std, W1_words, W1_sc
         c_sb = [keep.tile([P, D_OUT], F32, name="c_sb%d" % tt) for tt in range(NT)]
 
         nc.gpsimd.memset(vrows[:].bitcast(F32), 0.0)
+        nc.vector.memset(end_rows[:].bitcast(I32), 0)
         nc.vector.memset(rows2[:].bitcast(I32), 0)
         nc.vector.memset(w1sr[:, 0:512].bitcast(I32), 0)
         nc.vector.memset(warm[:], 1.0)
         nc.vector.memset(w1sr[:, 512:2048].bitcast(I32), 0)
         nc.vector.memset(w2s[:].bitcast(I32), 0)
-        nc.vector.memset(end_rows[:].bitcast(I32), 0)
         make_identity(nc, ident_f[:])
+        nc.gpsimd.dma_start(out=vrows[0:NG, :], in_=b1.rearrange("(g k) -> g k", g=NG))
         nc.vector.tensor_copy(out=ident_b[:], in_=ident_f[:])
 
         idle = psum.tile([P, 512], F32, name="idle", tag="acc0")
         for i in range(4):
-            nc.tensor.matmul(out=idle[:], lhsT=vrows[:, 0:P], rhs=vrows[:], start=True, stop=True)
+            nc.tensor.matmul(out=idle[:], lhsT=end_rows[:, 0:P], rhs=end_rows[:], start=True, stop=True)
 
         with nc.allow_non_contiguous_dma(reason="four neighbouring elements to a partition"):
             nc.scalar.dma_start(out=std4[:], in_=in_std.rearrange("(p t) -> p t", t=4))
             nc.scalar.dma_start(out=mean4[:], in_=in_mean.rearrange("(p t) -> p t", t=4))
         nc.sync.dma_start(out=x_sb[:], in_=x.rearrange("(tt p) k -> p tt k", p=P))
-        nc.scalar.activation(out=warm2[:], in_=warm[:], func=ACT.Abs_reciprocal_sqrt)
 
         w1_dram = W1_words[0].rearrange("p n t -> p (n t)")
 
@@ -94,9 +94,9 @@ def tile_mlp_w_kernel(tc, x, in_mean, in_std, out_mean, out_std, W1_words, W1_sc
             nc.sync.dma_start(out=w2[:, 2 * i:2 * i + 2, :].bitcast(I32),
                               in_=W2_words[2 * i:2 * i + 2].rearrange("g p n t -> p g (n t)").bitcast(I32))
 
-        def load_w1s(j0, j1, g0, quadrants):
+        def load_w1s(j0, j1, g0):
             n = 512 * (j1 - j0)
-            for q in quadrants:
+            for q in range(4):
                 nc.sync.dma_start(
                     out=w1sr[32 * q:32 * q + 16, 512 * j0:512 * j1].bitcast(I32),
                     in_=W1_scales[0, 4 * q:4 * q + 4, 512 * g0:512 * g0 + 4 * n].rearrange("r (c n) -> c r n", c=4).bitcast(I32))
@@ -111,15 +111,14 @@ def tile_mlp_w_kernel(tc, x, in_mean, in_std, out_mean, out_std, W1_words, W1_sc
             for r, v in enumerate((b2, out_std)):
                 nc.sync.dma_start(out=end_rows[r:r + 1, :], in_=v.unsqueeze(0))
 
-        load_w1(0, 1)
+        load_w1(0, 2)
         for r, v in enumerate((in_mean, out_mean)):
-            nc.sync.dma_start(out=rows2[r:r + 1, :], in_=v.unsqueeze(0))
-        load_w1s(0, 1, 0, range(4))
-        nc.sync.dma_start(out=vrows[0:NG, :], in_=b1.rearrange("(g k) -> g k", g=NG))
-        load_w1(1, 2)
+            nc.scalar.dma_start(out=rows2[r:r + 1, :], in_=v.unsqueeze(0))
+        nc.scalar.activation(out=warm2[:], in_=warm[:], func=ACT.Abs_reciprocal_sqrt)
+        load_w1s(0, 1, 0)
         load_w1(2, 4)
-        load_w1s(1, 4, 4, range(4))
         load_w1(4, 6)
+        load_w1s(1, 4, 4)
         load_w1(6, 8)
         load_w2s(0)
         load_w2(0)
@@ -159,17 +158,17 @@ def tile_mlp_w_kernel(tc, x, in_mean, in_std, out_mean, out_std, W1_words, W1_sc
         for tt in range(NT):
             for u in range(2):
                 nc.tensor.transpose(out=xT[tt][u][:], in_=x_sb[:, tt, :].bitcast(F32)[:, u:256:2], identity=ident_f[:])
-        permute(UNITS[0])
         for tt in range(NT):
-            for t in range(4):
+            for t in (0, 2, 3, 1):
                 src = xT[tt][t // 2][:].bitcast(BF16).rearrange("p (k e) -> p e k", e=2)[:, t % 2]
                 dst = xs[tt][:, t, :]
-                if t < 2:
+                if t == 0:
                     nc.vector.tensor_scalar(out=dst, in0=src, scalar1=meanf[:, t:t + 1],
                                             scalar2=rstd4[:, t:t + 1], op0=ALU.subtract, op1=ALU.mult)
                 else:
                     nc.scalar.activation(out=dst, in_=src, func=ACT.Identity,
                                          scale=rstd4[:, t:t + 1], bias=nmr4[:, t:t + 1])
+        permute(UNITS[0])
         for tt in range(NT):
             nc.vector.tensor_copy(out=xg[:, 512 * tt:512 * (tt + 1)].rearrange("p (c i t) -> p c t i", i=4, t=4),
                                   in_=xs[tt][:].rearrange("p t (c i) -> p c t i", i=4))
@@ -182,6 +181,12 @@ def tile_mlp_w_kernel(tc, x, in_mean, in_std, out_mean, out_std, W1_words, W1_sc
             nc.tensor.matmul(out=ps_c[tt][:], lhsT=ident_b[:], rhs=x_sb[:, tt, :], start=True, stop=False)
         for tt in range(NT):
             nc.tensor.matmul(out=ps_c[tt][:], lhsT=dvec[:, 0:1].to_broadcast([P, P]), rhs=rows2[:], start=False, stop=True)
+        def idle_products(tag, n):
+            idle = psum.tile([P, 512], F32, name="idle_" + tag, tag=tag)
+            for i in range(n):
+                nc.tensor.matmul(out=idle[:], lhsT=ident_b[:], rhs=x_sb[:, 0, :], start=True, stop=True)
+
+        idle_products("l1_1", 3)
         bT = psum.tile([P, 2, P], F32, name="bT", tag="l1_0")
         for u in range(2):
             nc.tensor.transpose(out=bT[:, u, :], in_=vrows[:].bitcast(F32)[:, u:256:2], identity=ident_f[:])
@@ -252,7 +257,6 @@ def tile_mlp_w_kernel(tc, x, in_mean, in_std, out_mean, out_std, W1_words, W1_sc
                                         start=(g == 0), stop=(g == NG - 1))
 
         NK = len(PARTS)
-        LAST = NK - 1 - NT
         for k in range(NK + LAG):
             if k < NK:
                 evacuate(k)
@@ -266,16 +270,17 @@ def tile_mlp_w_kernel(tc, x, in_mean, in_std, out_mean, out_std, W1_words, W1_sc
             if 1 <= k <= NK:
                 interleave(k - 1)
             if k == 1:
-                permute_scales(1, 2)
                 quantise(0)
             if k == 2:
                 permute_scales(2, 4)
             if k + LEAD < len(UNITS):
                 permute(UNITS[k + LEAD])
-            if 1 < k <= LAST:
+            if k == 1:
+                permute_scales(1, 2)
+            if 2 <= k <= NK:
                 quantise(k - 1)
-            if LAST <= k - 2 < NK:
-                quantise(k - 2)
+            if k == LAG:
+                idle_products("acc1", 2)
             if k >= LAG:
                 layer2(k - LAG)
 

from contextlib import ExitStack

import concourse.mybir as mybir
from concourse.masks import make_identity

F32 = mybir.dt.float32
BF16 = mybir.dt.bfloat16
I32 = mybir.dt.int32
U32 = mybir.dt.uint32
U8 = mybir.dt.uint8
FP8X4 = mybir.dt.float8_e4m3fn_x4
ALU = mybir.AluOpType
ACT = mybir.ActivationFunctionType

P = 128
B, D_IN, D_HID, D_OUT = 256, 512, 8192, 512
NT = B // P
NG = D_HID // 512
EPS = 1e-12
FLOPS = 2 * B * D_IN * D_HID + 2 * B * D_HID * D_OUT
UNITS = [[0], [1]] + [[g, g + 1] for g in range(2, NG - 2, 2)] + [[NG - 2], [NG - 1]]
PARTS = [(u, 0, B) for u in UNITS[:-1]] + [(UNITS[-1], P * tt, P * (tt + 1)) for tt in range(NT)]
LEAD = 2
LAG = 2


def tile_mlp_w_kernel(tc, x, in_mean, in_std, out_mean, out_std, W1_words, W1_scales, b1,
                                 W2_words, W2_scales, b2, norm_max, out):
    nc = tc.nc
    with ExitStack() as ctx:
        keep = ctx.enter_context(tc.tile_pool(name="keep", bufs=1))
        spool = ctx.enter_context(tc.tile_pool(name="spool", bufs=3))
        gpool = ctx.enter_context(tc.tile_pool(name="gpool", bufs=3))
        psum = ctx.enter_context(tc.psum_pool(name="psum", bufs=1))
        ctx.enter_context(tc.manual_schedule())

        x_sb = keep.tile([P, NT, D_IN], BF16, name="x_sb")
        mean4 = keep.tile([P, 4], BF16, name="mean4")
        std4 = keep.tile([P, 4], BF16, name="std4")
        rstd4 = keep.tile([P, 4], F32, name="rstd4")
        meanf = keep.tile([P, 4], F32, name="meanf")
        nmr4 = keep.tile([P, 4], F32, name="nmr4")
        ident_f = keep.tile([P, P], F32, name="ident_f")
        ident_b = keep.tile([P, P], BF16, name="ident_b")
        dvec = keep.tile([P, 1], BF16, name="dvec")
        rows2 = keep.tile([P, 512], BF16, name="rows2")
        vrows = keep.tile([P, 512], BF16, name="vrows")
        w1r = keep.tile([P, D_HID], U32, name="w1r", align_bytes=64)
        w1p = keep.tile([P, D_HID], U32, name="w1p", align_bytes=64)
        w2 = keep.tile([P, NG, D_OUT], U32, name="w2", align_bytes=64)
        w1sr = keep.tile([P, 2048], U8, name="w1sr", align_bytes=64)
        w1sp = keep.tile([P, 2048], U8, name="w1sp", align_bytes=64)
        w2s = keep.tile([P, 2048], U8, name="w2s", align_bytes=64)
        b1t = keep.tile([P, NG, 4], BF16, name="b1t")
        xs = [keep.tile([P, 4, P], BF16, name="xs%d" % tt) for tt in range(NT)]
        xg = keep.tile([P, NT * 512], BF16, name="xg", align_bytes=64)
        xq = keep.tile([P, B], U32, name="xq", align_bytes=64)
        xqs = keep.tile([P, B], U8, name="xqs", align_bytes=64)
        hq = keep.tile([P, NG * B], U32, name="hq", align_bytes=64)
        hqs = keep.tile([P, NG * B], U8, name="hqs", align_bytes=64)
        warm = keep.tile([P, 1], F32, name="warm")
        warm2 = keep.tile([P, 1], F32, name="warm2")
        end_rows = keep.tile([P, D_OUT], BF16, name="end_rows")
        b2_bc = keep.tile([P, D_OUT], F32, name="b2_bc")
        c_sb = [keep.tile([P, D_OUT], F32, name="c_sb%d" % tt) for tt in range(NT)]

        nc.gpsimd.memset(vrows[:].bitcast(F32), 0.0)
        nc.vector.memset(end_rows[:].bitcast(I32), 0)
        nc.vector.memset(rows2[:].bitcast(I32), 0)
        nc.vector.memset(w1sr[:, 0:512].bitcast(I32), 0)
        nc.vector.memset(warm[:], 1.0)
        nc.vector.memset(w1sr[:, 512:2048].bitcast(I32), 0)
        nc.vector.memset(w2s[:].bitcast(I32), 0)
        make_identity(nc, ident_f[:])
        nc.gpsimd.dma_start(out=vrows[0:NG, :], in_=b1.rearrange("(g k) -> g k", g=NG))
        nc.vector.tensor_copy(out=ident_b[:], in_=ident_f[:])

        idle = psum.tile([P, 512], F32, name="idle", tag="acc0")
        for i in range(4):
            nc.tensor.matmul(out=idle[:], lhsT=end_rows[:, 0:P], rhs=end_rows[:], start=True, stop=True)

        with nc.allow_non_contiguous_dma(reason="four neighbouring elements to a partition"):
            nc.scalar.dma_start(out=std4[:], in_=in_std.rearrange("(p t) -> p t", t=4))
            nc.scalar.dma_start(out=mean4[:], in_=in_mean.rearrange("(p t) -> p t", t=4))
        nc.sync.dma_start(out=x_sb[:], in_=x.rearrange("(tt p) k -> p tt k", p=P))

        w1_dram = W1_words[0].rearrange("p n t -> p (n t)")

        def load_w1(g0, g1):
            nc.sync.dma_start(out=w1r[:, 512 * g0:512 * g1].bitcast(I32),
                              in_=w1_dram[:, 2048 * g0:2048 * g1].bitcast(I32))

        def load_w2(i):
            nc.sync.dma_start(out=w2[:, 2 * i:2 * i + 2, :].bitcast(I32),
                              in_=W2_words[2 * i:2 * i + 2].rearrange("g p n t -> p g (n t)").bitcast(I32))

        def load_w1s(j0, j1, g0):
            n = 512 * (j1 - j0)
            for q in range(4):
                nc.sync.dma_start(
                    out=w1sr[32 * q:32 * q + 16, 512 * j0:512 * j1].bitcast(I32),
                    in_=W1_scales[0, 4 * q:4 * q + 4, 512 * g0:512 * g0 + 4 * n].rearrange("r (c n) -> c r n", c=4).bitcast(I32))

        def load_w2s(b):
            for q in range(4):
                nc.sync.dma_start(
                    out=w2s[32 * q:32 * q + 16, 512 * b:512 * (b + 1)].bitcast(I32),
                    in_=W2_scales[4 * b:4 * b + 4, 4 * q:4 * q + 4, :].bitcast(I32))

        def load_end_rows():
            for r, v in enumerate((b2, out_std)):
                nc.sync.dma_start(out=end_rows[r:r + 1, :], in_=v.unsqueeze(0))

        load_w1(0, 2)
        for r, v in enumerate((in_mean, out_mean)):
            nc.scalar.dma_start(out=rows2[r:r + 1, :], in_=v.unsqueeze(0))
        nc.scalar.activation(out=warm2[:], in_=warm[:], func=ACT.Abs_reciprocal_sqrt)
        load_w1s(0, 1, 0)
        load_w1(2, 4)
        load_w1(4, 6)
        load_w1s(1, 4, 4)
        load_w1(6, 8)
        load_w2s(0)
        load_w2(0)
        load_w1(8, 10)
        load_w2(1)
        load_w1(10, 12)
        load_w2s(1)
        load_w2(2)
        load_w1(12, 14)
        load_w2(3)
        load_w1(14, 16)
        load_end_rows()
        load_w2s(2)
        load_w2(4)
        load_w2(5)
        load_w2s(3)
        load_w2(6)
        load_w2(7)

        def permute_scales(j0, j1):
            nc.vector.tensor_copy(out=w1sp[:].rearrange("p (t x i) -> p x t i", t=4, i=16)[:, 8 * j0:8 * j1],
                                  in_=w1sr[:, 512 * j0:512 * j1].rearrange("p (x i t) -> p x t i", i=16, t=4))

        def permute(unit):
            lo, hi = 512 * unit[0], 512 * (unit[-1] + 1)
            nc.vector.tensor_copy(
                out=w1p[:, lo:hi].bitcast(I32).rearrange("p (t c i) -> p c t i", t=4, i=4),
                in_=w1r[:, lo:hi].bitcast(I32).rearrange("p (c i t) -> p c t i", t=4, i=4))

        nc.vector.tensor_tensor(out=dvec[:], in0=ident_b[:, 1:2], in1=ident_b[:, 0:1], op=ALU.subtract)
        nc.vector.reciprocal(out=rstd4[:], in_=std4[:])
        nc.vector.tensor_copy(out=meanf[:], in_=mean4[:])
        nc.vector.scalar_tensor_tensor(out=nmr4[:], in0=meanf[:], scalar=-1.0, in1=rstd4[:], op0=ALU.mult, op1=ALU.mult)

        xT = [[psum.tile([P, P], F32, name="xT%d_%d" % (tt, u), tag="l1_%d" % (2 + 2 * tt + u)) for u in range(2)]
              for tt in range(NT)]
        for tt in range(NT):
            for u in range(2):
                nc.tensor.transpose(out=xT[tt][u][:], in_=x_sb[:, tt, :].bitcast(F32)[:, u:256:2], identity=ident_f[:])
        for tt in range(NT):
            for t in (0, 2, 3, 1):
                src = xT[tt][t // 2][:].bitcast(BF16).rearrange("p (k e) -> p e k", e=2)[:, t % 2]
                dst = xs[tt][:, t, :]
                if t == 0:
                    nc.vector.tensor_scalar(out=dst, in0=src, scalar1=meanf[:, t:t + 1],
                                            scalar2=rstd4[:, t:t + 1], op0=ALU.subtract, op1=ALU.mult)
                else:
                    nc.scalar.activation(out=dst, in_=src, func=ACT.Identity,
                                         scale=rstd4[:, t:t + 1], bias=nmr4[:, t:t + 1])
        permute(UNITS[0])
        for tt in range(NT):
            nc.vector.tensor_copy(out=xg[:, 512 * tt:512 * (tt + 1)].rearrange("p (c i t) -> p c t i", i=4, t=4),
                                  in_=xs[tt][:].rearrange("p t (c i) -> p c t i", i=4))
        permute_scales(0, 1)
        nc.vector.quantize_mx(out=xq[:].bitcast(FP8X4), scales=xqs[:], in_=xg[:])
        permute(UNITS[1])

        ps_c = [psum.tile([P, 512], F32, name="ps_c%d" % tt, tag="acc%d" % tt) for tt in range(NT)]
        for tt in range(NT):
            nc.tensor.matmul(out=ps_c[tt][:], lhsT=ident_b[:], rhs=x_sb[:, tt, :], start=True, stop=False)
        for tt in range(NT):
            nc.tensor.matmul(out=ps_c[tt][:], lhsT=dvec[:, 0:1].to_broadcast([P, P]), rhs=rows2[:], start=False, stop=True)
        def idle_products(tag, n):
            idle = psum.tile([P, 512], F32, name="idle_" + tag, tag=tag)
            for i in range(n):
                nc.tensor.matmul(out=idle[:], lhsT=ident_b[:], rhs=x_sb[:, 0, :], start=True, stop=True)

        idle_products("l1_1", 3)
        bT = psum.tile([P, 2, P], F32, name="bT", tag="l1_0")
        for u in range(2):
            nc.tensor.transpose(out=bT[:, u, :], in_=vrows[:].bitcast(F32)[:, u:256:2], identity=ident_f[:])
        b4 = bT[:].rearrange("p u r -> p (u r)").bitcast(BF16).rearrange("p (u r e) -> p r u e", u=2, e=2)
        for tt in range(NT):
            nc.scalar.copy(out=c_sb[tt][:], in_=ps_c[tt][:])
        nc.scalar.copy(out=b1t[:].rearrange("p g (u e) -> p g u e", u=2), in_=b4[:, 0:NG])

        l1_tiles = {}
        hs_tiles = {}
        hg_tiles = {}
        acc = []

        def layer1(unit, g):
            k = 4 * (g if g < 4 else (g - 4) // 3)
            c = P * (0 if g < 4 else 1 + (g - 4) % 3)
            for u in range(2):
                bank = psum.tile([P, 2, B], F32, name="l1_%d_%d" % (g, u), tag="l1_%d" % ((2 * g + u) % 6))
                l1_tiles[(g, u)] = bank
                for e in range(2):
                    t = 2 * u + e
                    col = 512 * unit[0] + P * (len(unit) * t + g - unit[0])
                    nc.tensor.matmul_mx(out=bank[:, e, :],
                                        lhsT=w1p[:, col:col + P].bitcast(FP8X4),
                                        lhsT_scale=w1sp[k:P, 512 * t + c:512 * t + c + P],
                                        rhs=xq[:].bitcast(FP8X4), rhs_scale=xqs[:], start=True, stop=True)

        def part_columns(k):
            units, lo, hi = PARTS[k]
            return B * units[0] + len(units) * lo, hi - lo

        def evacuate(k):
            groups, lo, hi = PARTS[k]
            n = hi - lo
            hs_tiles[k] = spool.tile([P, 4, len(groups) * n], BF16, name="hs_%d" % k, tag="hs")
            for j, g in enumerate(groups):
                if lo == 0:
                    layer1(groups, g)
                for t in range(4):
                    nc.scalar.activation(out=hs_tiles[k][:, t, n * j:n * (j + 1)], in_=l1_tiles[(g, t // 2)][:, t % 2, lo:hi],
                                         func=ACT.Relu, bias=b1t[:, g, t:t + 1])

        def interleave(k):
            groups, lo, hi = PARTS[k]
            hg = gpool.tile([P, len(groups) * 4 * (hi - lo)], BF16, name="hg_%d" % k, tag="hg", align_bytes=64)
            hg_tiles[k] = hg
            nc.vector.tensor_copy(out=hg[:].rearrange("p (c i t) -> p c t i", i=4, t=4),
                                  in_=hs_tiles[k][:].rearrange("p t (c i) -> p c t i", i=4))

        def quantise(k):
            c, n = part_columns(k)
            c1 = c + len(PARTS[k][0]) * n
            nc.vector.quantize_mx(out=hq[:, c:c1].bitcast(FP8X4), scales=hqs[:, c:c1], in_=hg_tiles[k][:])

        def layer2(k):
            groups, lo, hi = PARTS[k]
            c0, n = part_columns(k)
            for j, g in enumerate(groups):
                row = 4 * (g % 4)
                b = 512 * (g // 4)
                if g == 0:
                    for tt in range(NT):
                        acc.append(psum.tile([P, 512], F32, name="acc%d" % tt, tag="acc%d" % tt))
                for tt in range(lo // P, hi // P):
                    c = c0 + n * j + P * tt - lo
                    nc.tensor.matmul_mx(out=acc[tt][:], lhsT=hq[:, c:c + P].bitcast(FP8X4), lhsT_scale=hqs[:, c:c + P],
                                        rhs=w2[:, g, :].bitcast(FP8X4), rhs_scale=w2s[row:P, b:b + 512],
                                        start=(g == 0), stop=(g == NG - 1))

        NK = len(PARTS)
        for k in range(NK + LAG):
            if k < NK:
                evacuate(k)
            if k == NK - 2:
                spread = [psum.tile([P, D_OUT], F32, name="spread%d" % r, tag="l1_%d" % (2 + r)) for r in range(2)]
                for r in range(2):
                    nc.tensor.matmul(out=spread[r][:], lhsT=ident_b[:, r:r + 1].to_broadcast([P, P]), rhs=end_rows[:],
                                     start=True, stop=True)
            if k == NK - 1:
                nc.scalar.copy(out=b2_bc[:], in_=spread[0][:])
            if 1 <= k <= NK:
                interleave(k - 1)
            if k == 1:
                quantise(0)
            if k == 2:
                permute_scales(2, 4)
            if k + LEAD < len(UNITS):
                permute(UNITS[k + LEAD])
            if k == 1:
                permute_scales(1, 2)
            if 2 <= k <= NK:
                quantise(k - 1)
            if k == LAG:
                idle_products("acc1", 2)
            if k >= LAG:
                layer2(k - LAG)

        nm2 = float(norm_max) * float(norm_max)
        res, rr, mp, ot, junk = [], [], [], [], []
        n2, f0, fac, m2, r0, rinv = [], [], [], [], [], []
        for tt in range(NT):
            res.append(keep.tile([P, D_OUT], F32, name="res%d" % tt))
            rr.append(keep.tile([P, D_OUT], F32, name="rr%d" % tt))
            mp.append(keep.tile([P, D_OUT], F32, name="mp%d" % tt))
            ot.append(keep.tile([P, D_OUT], F32, name="ot%d" % tt))
            junk.append(keep.tile([P, D_OUT], F32, name="junk%d" % tt))
            for lst, nm in ((n2, "n2"), (f0, "f0"), (fac, "fac"), (m2, "m2"), (r0, "r0"), (rinv, "rinv")):
                lst.append(keep.tile([P, 1], F32, name="%s_%d" % (nm, tt)))

        m2b = keep.tile([P, 1], F32, name="m2b")

        def end_add(tt):
            nc.vector.tensor_tensor(out=res[tt][:], in0=acc[tt][:], in1=b2_bc[:], op=ALU.add)

        def end_norm1(tt):
            nc.scalar.activation(out=junk[tt][:], in_=res[tt][:], func=ACT.Square, accum_out=n2[tt][:])
            nc.scalar.activation(out=f0[tt][:], in_=n2[tt][:], func=ACT.Abs_reciprocal_sqrt, scale=1.0 / nm2)

        def end_gain(tt):
            nc.vector.tensor_tensor(out=rr[tt][:], in0=res[tt][:], in1=spread[1][:], op=ALU.mult)

        def end_clamp(tt):
            nc.vector.tensor_scalar_min(out=fac[tt][:], in0=f0[tt][:], scalar1=1.0)

        def end_map(tt):
            nc.vector.scalar_tensor_tensor(out=mp[tt][:], in0=rr[tt][:], scalar=fac[tt][:, 0:1], in1=c_sb[tt][:],
                                           op0=ALU.mult, op1=ALU.add)

        def end_norm2(tt):
            if tt == NT - 1:
                half = D_OUT // 2
                right = mp[tt][:, half:D_OUT]
                nc.vector.scalar_tensor_tensor(out=rr[tt][:, half:D_OUT], in0=right, scalar=1.0, in1=right,
                                               op0=ALU.mult, op1=ALU.mult, accum_out=m2b[:])
                nc.scalar.activation(out=junk[tt][:, 0:half], in_=mp[tt][:, 0:half], func=ACT.Square, accum_out=m2[tt][:])
                nc.scalar.activation(out=r0[tt][:], in_=m2[tt][:], func=ACT.Abs_reciprocal_sqrt, bias=m2b[:, 0:1])
            else:
                nc.scalar.activation(out=junk[tt][:], in_=mp[tt][:], func=ACT.Square, accum_out=m2[tt][:])
                nc.scalar.activation(out=r0[tt][:], in_=m2[tt][:], func=ACT.Abs_reciprocal_sqrt)

        def end_out(tt):
            nc.vector.tensor_scalar_min(out=rinv[tt][:], in0=r0[tt][:], scalar1=1.0 / EPS)
            nc.vector.tensor_scalar_mul(out=ot[tt][:], in0=mp[tt][:], scalar1=rinv[tt][:, 0:1])
            nc.sync.dma_start(out=out[P * tt:P * (tt + 1), :], in_=ot[tt][:])

        for tt in range(NT):
            end_add(tt)
        for tt in range(NT):
            end_norm1(tt)
        for tt in range(NT):
            end_gain(tt)
            end_clamp(tt)
        for stage in (end_map, end_norm2, end_out):
            for tt in range(NT):
                stage(tt)
